import numpy as np
import ml_dtypes


def mxq(x, axis, fmt="e4m3"):
    dtype, down = {"e4m3": (ml_dtypes.float8_e4m3fn, 7), "e5m2": (ml_dtypes.float8_e5m2, 14)}[fmt]
    v = np.moveaxis(np.asarray(x, np.float32).astype(ml_dtypes.bfloat16).astype(np.float64), axis, -1)
    blocks = v.reshape(v.shape[:-1] + (-1, 32))
    amax = np.abs(blocks).max(-1, keepdims=True)
    byte = np.maximum(np.where(amax > 0, np.frexp(amax)[1] - 1 + 127, 0) - down, 1)
    scale = np.exp2(byte - 127.0)
    codes = (blocks / scale).astype(np.float32).astype(dtype).astype(np.float64)
    return np.moveaxis((codes * scale).reshape(v.shape), -1, axis)


WIDE = False


def mx_kscale(k):
    if not WIDE:
        return np.ones(k)
    levels = np.array([10, -10, 5, -5, 0])
    a = np.random.permutation(np.resize(levels, k // 512 * 4)).reshape(k // 512, 4)
    idx = np.arange(k)
    return np.exp2(a[idx // 512, idx % 128 // 32])


BF16 = ml_dtypes.bfloat16


def bf(x):
    return np.asarray(x, np.float32).astype(BF16)


def f64(x):
    return np.asarray(x).astype(np.float64)


NI, NJ, NK, CZ, CM = 1024, 128, 512, 128, 16
EPS = 1e-5


def setup_inputs():
    s = mx_kscale(NK)[None, :, None]
    a = 1.2 / NK ** 0.25
    return {"left": bf(np.random.standard_normal((NI, NK, CM)) * a * s),
            "right": bf(np.random.standard_normal((NJ, NK, CM)) * a / s),
            "ln_c_w": bf(1.0 + 0.1 * np.random.standard_normal(CM)),
            "ln_c_b": bf(0.1 * np.random.standard_normal(CM))}


def reference(left, right, ln_c_w, ln_c_b):
    lq = mxq(f64(left).transpose(2, 0, 1), 2, "e4m3")
    rq = mxq(f64(right).transpose(2, 1, 0), 1, "e4m3")
    t = (lq @ rq).transpose(1, 2, 0)
    mu = t.mean(-1, keepdims=True)
    var = t.var(-1, keepdims=True)
    return (t - mu) * (1.0 / np.sqrt(var + EPS)) * f64(ln_c_w) + f64(ln_c_b)

@@ -1,0 +1,170 @@
+from contextlib import ExitStack
+
+import concourse.mybir as mybir
+from concourse.masks import make_identity
+
+F32 = mybir.dt.float32
+BF16 = mybir.dt.bfloat16
+U32 = mybir.dt.uint32
+U8 = mybir.dt.uint8
+FP8X4 = mybir.dt.float8_e4m3fn_x4
+ALU = mybir.AluOpType
+ACT = mybir.ActivationFunctionType
+
+NI, NJ, NK, CM = 1024, 128, 512, 16
+EPS = 1e-5
+P = 128
+PACK = 4
+CPAIRS = CM // 2
+ROW = NK * CM
+N_TILES = NI // P
+CHUNK_I = P // PACK
+CHUNKS = P // CHUNK_I
+CHUNK_COLS = ROW // PACK
+FLOPS = 2 * NI * NJ * NK * CM
+V_UNITS = {-1: 8, 0: 8, 1: 3, 2: 3, 3: 2, 4: 3, 5: 3, 6: 2, 7: 3}
+
+
+def tile_trianglemultiplication_pa_t_kernel(tc, left, right, ln_c_w, ln_c_b, out):
+    nc = tc.nc
+    with ExitStack() as ctx:
+        const = ctx.enter_context(tc.tile_pool(name="const", bufs=1))
+        xpool = ctx.enter_context(tc.tile_pool(name="xpool", bufs=12))
+        gpool = ctx.enter_context(tc.tile_pool(name="gpool", bufs=2))
+        cpool = ctx.enter_context(tc.tile_pool(name="cpool", bufs=2))
+        work = ctx.enter_context(tc.tile_pool(name="work", bufs=2))
+        small = ctx.enter_context(tc.tile_pool(name="small", bufs=2))
+        ps_tr = ctx.enter_context(tc.psum_pool(name="ps_tr", bufs=4))
+        ps_t = ctx.enter_context(tc.psum_pool(name="ps_t", bufs=2))
+        ps_s = ctx.enter_context(tc.psum_pool(name="ps_s", bufs=1))
+        ps_v = ctx.enter_context(tc.psum_pool(name="ps_v", bufs=1))
+
+        eps_t = const.tile([P, 1], F32)
+        nc.vector.memset(eps_t[:], EPS)
+        warm = const.tile([P, 1], F32)
+        nc.scalar.activation(out=warm[:], in_=eps_t[:], func=ACT.Sqrt)
+
+        ident = const.tile([P, P], F32)
+        make_identity(nc, ident[:])
+
+        w16 = const.tile([P, CM], BF16)
+        b16 = const.tile([P, CM], BF16)
+        nc.gpsimd.dma_start(out=w16[:], in_=ln_c_w.partition_broadcast(P))
+        nc.gpsimd.dma_start(out=b16[:], in_=ln_c_b.partition_broadcast(P))
+        w32 = const.tile([P, CM], F32)
+        b32 = const.tile([P, CM], F32)
+        nc.vector.tensor_copy(out=w32[:], in_=w16[:])
+        nc.vector.tensor_copy(out=b32[:], in_=b16[:])
+
+        r_codes = const.tile([P, CM * P], U32, align_bytes=64)
+        r_scales = const.tile([P, CM * P], U8, align_bytes=64)
+
+        def quantise(rows, codes, scales, n_vector):
+            grouped = gpool.tile([P, ROW], BF16, name="grouped", align_bytes=64)
+            by_channel = grouped[:].rearrange("p (c x) -> p c x", c=CM)
+            unit = 0
+            for g in range(CHUNKS):
+                x = xpool.tile([P, CHUNK_COLS], BF16, name="x")
+                nc.sync.dma_start(
+                    out=x[:],
+                    in_=rows[g * CHUNK_I:(g + 1) * CHUNK_I].rearrange(
+                        "i (t p) c -> (i t) (p c)", t=PACK))
+                words = x[:].bitcast(F32).rearrange("r (p q) -> r q p", q=CPAIRS)
+                for hb in range(2):
+                    bank = ps_tr.tile([P, 4 * P], F32, name="bank")
+                    for ql in range(4):
+                        nc.tensor.transpose(
+                            bank[:, ql * P:(ql + 1) * P], words[:, 4 * hb + ql, :], ident[:])
+                    src = bank[:].bitcast(BF16).rearrange("p (q r e) -> p q e r", q=4, e=2)
+                    dst = by_channel[:, 8 * hb:8 * hb + 8, g * P:(g + 1) * P].rearrange(
+                        "p (q e) r -> p q e r", e=2)
+                    for hq in range(2):
+                        on_vector = (unit * n_vector) // 16 != ((unit + 1) * n_vector) // 16
+                        unit += 1
+                        if on_vector:
+                            nc.vector.tensor_copy(
+                                out=dst[:, 2 * hq:2 * hq + 2], in_=src[:, 2 * hq:2 * hq + 2])
+                        else:
+                            nc.scalar.copy(
+                                out=dst[:, 2 * hq:2 * hq + 2], in_=src[:, 2 * hq:2 * hq + 2])
+            half = ROW // 2
+            for h in range(2):
+                nc.vector.quantize_mx(
+                    out=codes[:, h * half // PACK:(h + 1) * half // PACK].bitcast(FP8X4),
+                    scales=scales[:, h * half // PACK:(h + 1) * half // PACK],
+                    in_=grouped[:, h * half:(h + 1) * half],
+                )
+
+        def mx(acc, l_codes, l_scales, c, start, stop):
+            cols = slice(c * P, (c + 1) * P)
+            nc.tensor.matmul_mx(
+                out=acc,
+                lhsT=l_codes[:, cols].bitcast(FP8X4),
+                lhsT_scale=l_scales[:, cols],
+                rhs=r_codes[:, cols].bitcast(FP8X4),
+                rhs_scale=r_scales[:, cols],
+                start=start,
+                stop=stop,
+            )
+
+        def finish(it, l_codes, l_scales):
+            total = ps_s.tile([P, P], F32, name="total")
+            for c in range(CM):
+                mx(total[:], l_codes, l_scales, c, c == 0, c == CM - 1)
+            mu = small.tile([P, P], F32, name="mu")
+            nc.scalar.mul(out=mu[:], in_=total[:], mul=1.0 / CM)
+            d = work.tile([P, CM * P], F32, name="d")
+            sq = work.tile([P, CM * P], F32, name="sq")
+            for b in range(4):
+                t_bank = ps_t.tile([P, 4 * P], F32, name="t_bank")
+                for cc in range(4):
+                    mx(t_bank[:, cc * P:(cc + 1) * P], l_codes, l_scales, 4 * b + cc, True, True)
+                cols = slice(b * 4 * P, (b + 1) * 4 * P)
+                nc.vector.tensor_tensor(
+                    out=d[:, cols].rearrange("p (c j) -> p c j", c=4),
+                    in0=t_bank[:].rearrange("p (c j) -> p c j", c=4),
+                    in1=mu[:].unsqueeze(1).to_broadcast([P, 4, P]),
+                    op=ALU.subtract,
+                )
+                nc.scalar.activation(out=sq[:, cols], in_=d[:, cols], func=ACT.Square)
+            s2ps = ps_v.tile([P, 2 * P], F32, name="s2ps")
+            for c in range(CM):
+                nc.tensor.matmul(
+                    out=s2ps[:, 0:P], lhsT=sq[:, c * P:(c + 1) * P], rhs=ident[:],
+                    start=(c == 0), stop=(c == CM - 1), is_transpose=True)
+            s2t = small.tile([P, P], F32, name="s2t")
+            nc.scalar.copy(out=s2t[:], in_=s2ps[:, 0:P])
+            nc.tensor.transpose(s2ps[:, P:2 * P], s2t[:], ident[:])
+            std = small.tile([P, P], F32, name="std")
+            nc.scalar.activation(
+                out=std[:], in_=s2ps[:, P:2 * P], func=ACT.Sqrt, bias=eps_t[:], scale=1.0 / CM)
+            rstd = small.tile([P, P], F32, name="rstd")
+            nc.vector.reciprocal(out=rstd[:], in_=std[:])
+            e = work.tile([P, CM * P], F32, name="e")
+            for c in range(CM):
+                cols = slice(c * P, (c + 1) * P)
+                nc.vector.scalar_tensor_tensor(
+                    out=e[:, cols], in0=d[:, cols], scalar=w32[:, c:c + 1], in1=rstd[:],
+                    op0=ALU.mult, op1=ALU.mult)
+            o = work.tile([P, P * CM], F32, name="o")
+            nc.gpsimd.tensor_tensor(
+                out=o[:].rearrange("p (j c) -> p j c", c=CM),
+                in0=e[:].rearrange("p (c j) -> p j c", c=CM),
+                in1=b32[:].unsqueeze(1).to_broadcast([P, P, CM]),
+                op=ALU.add,
+            )
+            nc.sync.dma_start(
+                out=out[it * P:(it + 1) * P].rearrange("i j c -> i (j c)"), in_=o[:])
+
+        def prepare(it):
+            l_codes = cpool.tile([P, CM * P], U32, name="l_codes", align_bytes=64)
+            l_scales = cpool.tile([P, CM * P], U8, name="l_scales", align_bytes=64)
+            quantise(left[it * P:(it + 1) * P], l_codes, l_scales, V_UNITS[it])
+            return l_codes, l_scales
+
+        quantise(right, r_codes, r_scales, V_UNITS[-1])
+        ready = prepare(0)
+        for it in range(N_TILES):
+            following = prepare(it + 1) if it + 1 < N_TILES else None
+            finish(it, ready[0], ready[1])
+            ready = following

@@ -15,35 +15,36 @@ NI, NJ, NK, CM = 1024, 128, 512, 16
 EPS = 1e-5
 P = 128
 PACK = 4
-CPAIRS = CM // 2
 ROW = NK * CM
 N_TILES = NI // P
 CHUNK_I = P // PACK
 CHUNKS = P // CHUNK_I
 CHUNK_COLS = ROW // PACK
 FLOPS = 2 * NI * NJ * NK * CM
-V_UNITS = {-1: 8, 0: 8, 1: 3, 2: 3, 3: 2, 4: 3, 5: 3, 6: 2, 7: 3}
+V_BANKS = [4, 4, 0, 0, 0, 0, 0, 0, 0]
+FINAL_V_COLS = 64
 
 
 def tile_trianglemultiplication_pa_t_kernel(tc, left, right, ln_c_w, ln_c_b, out):
     nc = tc.nc
     with ExitStack() as ctx:
         const = ctx.enter_context(tc.tile_pool(name="const", bufs=1))
-        xpool = ctx.enter_context(tc.tile_pool(name="xpool", bufs=12))
+        xpool = ctx.enter_context(tc.tile_pool(name="xpool", bufs=8))
         gpool = ctx.enter_context(tc.tile_pool(name="gpool", bufs=2))
         cpool = ctx.enter_context(tc.tile_pool(name="cpool", bufs=2))
         work = ctx.enter_context(tc.tile_pool(name="work", bufs=2))
         small = ctx.enter_context(tc.tile_pool(name="small", bufs=2))
-        ps_tr = ctx.enter_context(tc.psum_pool(name="ps_tr", bufs=4))
-        ps_t = ctx.enter_context(tc.psum_pool(name="ps_t", bufs=2))
-        ps_s = ctx.enter_context(tc.psum_pool(name="ps_s", bufs=1))
-        ps_v = ctx.enter_context(tc.psum_pool(name="ps_v", bufs=1))
+        ps_tr = ctx.enter_context(tc.psum_pool(name="ps_tr", bufs=3))
+        ps_t = ctx.enter_context(tc.psum_pool(name="ps_t", bufs=3))
+        ps_s = ctx.enter_context(tc.psum_pool(name="ps_s", bufs=2))
 
         eps_t = const.tile([P, 1], F32)
         nc.vector.memset(eps_t[:], EPS)
         warm = const.tile([P, 1], F32)
         nc.scalar.activation(out=warm[:], in_=eps_t[:], func=ACT.Sqrt)
 
+        ident_bf = const.tile([P, P], BF16)
+        make_identity(nc, ident_bf[:])
         ident = const.tile([P, P], F32)
         make_identity(nc, ident[:])
 
@@ -69,24 +70,20 @@ def tile_trianglemultiplication_pa_t_kernel(tc, left, right, ln_c_w, ln_c_b, out
                     out=x[:],
                     in_=rows[g * CHUNK_I:(g + 1) * CHUNK_I].rearrange(
                         "i (t p) c -> (i t) (p c)", t=PACK))
-                words = x[:].bitcast(F32).rearrange("r (p q) -> r q p", q=CPAIRS)
+                channel = x[:].rearrange("r (p c) -> r c p", c=CM)
                 for hb in range(2):
-                    bank = ps_tr.tile([P, 4 * P], F32, name="bank")
-                    for ql in range(4):
+                    bank = ps_tr.tile([P, 8 * P], BF16, name="bank")
+                    for cl in range(8):
                         nc.tensor.transpose(
-                            bank[:, ql * P:(ql + 1) * P], words[:, 4 * hb + ql, :], ident[:])
-                    src = bank[:].bitcast(BF16).rearrange("p (q r e) -> p q e r", q=4, e=2)
-                    dst = by_channel[:, 8 * hb:8 * hb + 8, g * P:(g + 1) * P].rearrange(
-                        "p (q e) r -> p q e r", e=2)
-                    for hq in range(2):
-                        on_vector = (unit * n_vector) // 16 != ((unit + 1) * n_vector) // 16
-                        unit += 1
-                        if on_vector:
-                            nc.vector.tensor_copy(
-                                out=dst[:, 2 * hq:2 * hq + 2], in_=src[:, 2 * hq:2 * hq + 2])
-                        else:
-                            nc.scalar.copy(
-                                out=dst[:, 2 * hq:2 * hq + 2], in_=src[:, 2 * hq:2 * hq + 2])
+                            bank[:, cl * P:(cl + 1) * P], channel[:, 8 * hb + cl, :], ident_bf[:])
+                    src = bank[:].rearrange("p (c r) -> p c r", c=8)
+                    dst = by_channel[:, 8 * hb:8 * hb + 8, g * P:(g + 1) * P]
+                    on_vector = (unit * n_vector) // 8 != ((unit + 1) * n_vector) // 8
+                    unit += 1
+                    if on_vector:
+                        nc.vector.tensor_copy(out=dst, in_=src)
+                    else:
+                        nc.scalar.copy(out=dst, in_=src)
             half = ROW // 2
             for h in range(2):
                 nc.vector.quantize_mx(
@@ -108,11 +105,12 @@ def tile_trianglemultiplication_pa_t_kernel(tc, left, right, ln_c_w, ln_c_b, out
             )
 
         def finish(it, l_codes, l_scales):
-            total = ps_s.tile([P, P], F32, name="total")
+            stat = ps_s.tile([P, 3 * P], F32, name="stat")
+            total = stat[:, 0:P]
             for c in range(CM):
-                mx(total[:], l_codes, l_scales, c, c == 0, c == CM - 1)
+                mx(total, l_codes, l_scales, c, c == 0, c == CM - 1)
             mu = small.tile([P, P], F32, name="mu")
-            nc.scalar.mul(out=mu[:], in_=total[:], mul=1.0 / CM)
+            nc.scalar.mul(out=mu[:], in_=total, mul=1.0 / CM)
             d = work.tile([P, CM * P], F32, name="d")
             sq = work.tile([P, CM * P], F32, name="sq")
             for b in range(4):
@@ -127,17 +125,16 @@ def tile_trianglemultiplication_pa_t_kernel(tc, left, right, ln_c_w, ln_c_b, out
                     op=ALU.subtract,
                 )
                 nc.scalar.activation(out=sq[:, cols], in_=d[:, cols], func=ACT.Square)
-            s2ps = ps_v.tile([P, 2 * P], F32, name="s2ps")
             for c in range(CM):
                 nc.tensor.matmul(
-                    out=s2ps[:, 0:P], lhsT=sq[:, c * P:(c + 1) * P], rhs=ident[:],
+                    out=stat[:, P:2 * P], lhsT=sq[:, c * P:(c + 1) * P], rhs=ident[:],
                     start=(c == 0), stop=(c == CM - 1), is_transpose=True)
             s2t = small.tile([P, P], F32, name="s2t")
-            nc.scalar.copy(out=s2t[:], in_=s2ps[:, 0:P])
-            nc.tensor.transpose(s2ps[:, P:2 * P], s2t[:], ident[:])
+            nc.scalar.copy(out=s2t[:], in_=stat[:, P:2 * P])
+            nc.tensor.transpose(stat[:, 2 * P:3 * P], s2t[:], ident[:])
             std = small.tile([P, P], F32, name="std")
             nc.scalar.activation(
-                out=std[:], in_=s2ps[:, P:2 * P], func=ACT.Sqrt, bias=eps_t[:], scale=1.0 / CM)
+                out=std[:], in_=stat[:, 2 * P:3 * P], func=ACT.Sqrt, bias=eps_t[:], scale=1.0 / CM)
             rstd = small.tile([P, P], F32, name="rstd")
             nc.vector.reciprocal(out=rstd[:], in_=std[:])
             e = work.tile([P, CM * P], F32, name="e")
@@ -147,22 +144,27 @@ def tile_trianglemultiplication_pa_t_kernel(tc, left, right, ln_c_w, ln_c_b, out
                     out=e[:, cols], in0=d[:, cols], scalar=w32[:, c:c + 1], in1=rstd[:],
                     op0=ALU.mult, op1=ALU.mult)
             o = work.tile([P, P * CM], F32, name="o")
-            nc.gpsimd.tensor_tensor(
-                out=o[:].rearrange("p (j c) -> p j c", c=CM),
-                in0=e[:].rearrange("p (c j) -> p j c", c=CM),
-                in1=b32[:].unsqueeze(1).to_broadcast([P, P, CM]),
-                op=ALU.add,
-            )
+            o_jc = o[:].rearrange("p (j c) -> p j c", c=CM)
+            e_jc = e[:].rearrange("p (c j) -> p j c", c=CM)
+            fv = FINAL_V_COLS
+            if fv > 0:
+                nc.vector.tensor_tensor(
+                    out=o_jc[:, 0:fv], in0=e_jc[:, 0:fv],
+                    in1=b32[:].unsqueeze(1).to_broadcast([P, fv, CM]), op=ALU.add)
+            if fv < P:
+                nc.gpsimd.tensor_tensor(
+                    out=o_jc[:, fv:P], in0=e_jc[:, fv:P],
+                    in1=b32[:].unsqueeze(1).to_broadcast([P, P - fv, CM]), op=ALU.add)
             nc.sync.dma_start(
                 out=out[it * P:(it + 1) * P].rearrange("i j c -> i (j c)"), in_=o[:])
 
         def prepare(it):
             l_codes = cpool.tile([P, CM * P], U32, name="l_codes", align_bytes=64)
             l_scales = cpool.tile([P, CM * P], U8, name="l_scales", align_bytes=64)
-            quantise(left[it * P:(it + 1) * P], l_codes, l_scales, V_UNITS[it])
+            quantise(left[it * P:(it + 1) * P], l_codes, l_scales, V_BANKS[it + 1])
             return l_codes, l_scales
 
-        quantise(right, r_codes, r_scales, V_UNITS[-1])
+        quantise(right, r_codes, r_scales, V_BANKS[0])
         ready = prepare(0)
         for it in range(N_TILES):
             following = prepare(it + 1) if it + 1 < N_TILES else None

@@ -15,158 +15,241 @@ NI, NJ, NK, CM = 1024, 128, 512, 16
 EPS = 1e-5
 P = 128
 PACK = 4
+CPAIRS = CM // 2
 ROW = NK * CM
 N_TILES = NI // P
+N_UNITS = N_TILES + 1
 CHUNK_I = P // PACK
 CHUNKS = P // CHUNK_I
 CHUNK_COLS = ROW // PACK
+BANKS = 2 * CHUNKS
 FLOPS = 2 * NI * NJ * NK * CM
-V_BANKS = [4, 4, 0, 0, 0, 0, 0, 0, 0]
-FINAL_V_COLS = 64
 
 
 def tile_trianglemultiplication_pa_t_kernel(tc, left, right, ln_c_w, ln_c_b, out):
     nc = tc.nc
     with ExitStack() as ctx:
         const = ctx.enter_context(tc.tile_pool(name="const", bufs=1))
-        xpool = ctx.enter_context(tc.tile_pool(name="xpool", bufs=8))
+        xpool = ctx.enter_context(tc.tile_pool(name="xpool", bufs=12))
         gpool = ctx.enter_context(tc.tile_pool(name="gpool", bufs=2))
         cpool = ctx.enter_context(tc.tile_pool(name="cpool", bufs=2))
         work = ctx.enter_context(tc.tile_pool(name="work", bufs=2))
         small = ctx.enter_context(tc.tile_pool(name="small", bufs=2))
-        ps_tr = ctx.enter_context(tc.psum_pool(name="ps_tr", bufs=3))
+        ps_tr = ctx.enter_context(tc.psum_pool(name="ps_tr", bufs=4))
         ps_t = ctx.enter_context(tc.psum_pool(name="ps_t", bufs=3))
-        ps_s = ctx.enter_context(tc.psum_pool(name="ps_s", bufs=2))
+        ps_s = ctx.enter_context(tc.psum_pool(name="ps_s", bufs=1))
+        ctx.enter_context(tc.manual_schedule())
 
+        w16 = const.tile([P, CM], BF16)
+        b16 = const.tile([P, CM], BF16)
+        nc.scalar.dma_start(out=w16[:], in_=ln_c_w.partition_broadcast(P))
+        nc.scalar.dma_start(out=b16[:], in_=ln_c_b.partition_broadcast(P))
         eps_t = const.tile([P, 1], F32)
         nc.vector.memset(eps_t[:], EPS)
         warm = const.tile([P, 1], F32)
         nc.scalar.activation(out=warm[:], in_=eps_t[:], func=ACT.Sqrt)
-
-        ident_bf = const.tile([P, P], BF16)
-        make_identity(nc, ident_bf[:])
         ident = const.tile([P, P], F32)
         make_identity(nc, ident[:])
-
-        w16 = const.tile([P, CM], BF16)
-        b16 = const.tile([P, CM], BF16)
-        nc.gpsimd.dma_start(out=w16[:], in_=ln_c_w.partition_broadcast(P))
-        nc.gpsimd.dma_start(out=b16[:], in_=ln_c_b.partition_broadcast(P))
         w32 = const.tile([P, CM], F32)
         b32 = const.tile([P, CM], F32)
         nc.vector.tensor_copy(out=w32[:], in_=w16[:])
         nc.vector.tensor_copy(out=b32[:], in_=b16[:])
 
-        r_codes = const.tile([P, CM * P], U32, align_bytes=64)
-        r_scales = const.tile([P, CM * P], U8, align_bytes=64)
+        x_t = {}
+        bank_t = {}
+        grouped_t = {}
+        codes_t = {}
+        scales_t = {}
+        stat_t = {}
+        tb_t = {}
+        sb = {}
 
-        def quantise(rows, codes, scales, n_vector):
-            grouped = gpool.tile([P, ROW], BF16, name="grouped", align_bytes=64)
-            by_channel = grouped[:].rearrange("p (c x) -> p c x", c=CM)
-            unit = 0
+        def load(u):
+            if u >= N_UNITS:
+                return
+            rows = right if u == 0 else left[(u - 1) * P:u * P]
             for g in range(CHUNKS):
                 x = xpool.tile([P, CHUNK_COLS], BF16, name="x")
                 nc.sync.dma_start(
                     out=x[:],
                     in_=rows[g * CHUNK_I:(g + 1) * CHUNK_I].rearrange(
                         "i (t p) c -> (i t) (p c)", t=PACK))
-                channel = x[:].rearrange("r (p c) -> r c p", c=CM)
-                for hb in range(2):
-                    bank = ps_tr.tile([P, 8 * P], BF16, name="bank")
-                    for cl in range(8):
-                        nc.tensor.transpose(
-                            bank[:, cl * P:(cl + 1) * P], channel[:, 8 * hb + cl, :], ident_bf[:])
-                    src = bank[:].rearrange("p (c r) -> p c r", c=8)
-                    dst = by_channel[:, 8 * hb:8 * hb + 8, g * P:(g + 1) * P]
-                    on_vector = (unit * n_vector) // 8 != ((unit + 1) * n_vector) // 8
-                    unit += 1
-                    if on_vector:
-                        nc.vector.tensor_copy(out=dst, in_=src)
-                    else:
-                        nc.scalar.copy(out=dst, in_=src)
+                x_t[(u, g)] = x
+
+        def tr(u, banks):
+            if u >= N_UNITS:
+                return
+            for b in banks:
+                g, hb = b // 2, b % 2
+                words = x_t[(u, g)][:].bitcast(F32).rearrange("r (p q) -> r q p", q=CPAIRS)
+                bank = ps_tr.tile([P, 4 * P], F32, name="bank")
+                for ql in range(4):
+                    nc.tensor.transpose(
+                        bank[:, ql * P:(ql + 1) * P], words[:, 4 * hb + ql, :], ident[:])
+                bank_t[(u, b)] = bank
+
+        def co(u, banks):
+            if u >= N_UNITS:
+                return
+            for b in banks:
+                g, hb = b // 2, b % 2
+                if u not in grouped_t:
+                    grouped_t[u] = gpool.tile([P, ROW], BF16, name="grouped", align_bytes=64)
+                by_channel = grouped_t[u][:].rearrange("p (c x) -> p c x", c=CM)
+                src = bank_t[(u, b)][:].bitcast(BF16).rearrange("p (q r e) -> p q e r", q=4, e=2)
+                dst = by_channel[:, 8 * hb:8 * hb + 8, g * P:(g + 1) * P].rearrange(
+                    "p (q e) r -> p q e r", e=2)
+                on_vector = (b % 2 == 1) if u < 2 else (b in (5, 7))
+                if on_vector:
+                    nc.vector.tensor_copy(out=dst, in_=src)
+                else:
+                    nc.scalar.copy(out=dst, in_=src)
+
+        def quant(u):
+            if u >= N_UNITS:
+                return
+            pool = const if u == 0 else cpool
+            codes = pool.tile([P, CM * P], U32, name="codes" if u else "r_codes", align_bytes=64)
+            scales = pool.tile([P, CM * P], U8, name="scales" if u else "r_scales", align_bytes=64)
+            codes_t[u] = codes
+            scales_t[u] = scales
             half = ROW // 2
             for h in range(2):
                 nc.vector.quantize_mx(
                     out=codes[:, h * half // PACK:(h + 1) * half // PACK].bitcast(FP8X4),
                     scales=scales[:, h * half // PACK:(h + 1) * half // PACK],
-                    in_=grouped[:, h * half:(h + 1) * half],
+                    in_=grouped_t[u][:, h * half:(h + 1) * half],
                 )
 
-        def mx(acc, l_codes, l_scales, c, start, stop):
+        def mx(acc, n, c, start, stop):
             cols = slice(c * P, (c + 1) * P)
             nc.tensor.matmul_mx(
                 out=acc,
-                lhsT=l_codes[:, cols].bitcast(FP8X4),
-                lhsT_scale=l_scales[:, cols],
-                rhs=r_codes[:, cols].bitcast(FP8X4),
-                rhs_scale=r_scales[:, cols],
+                lhsT=codes_t[n + 1][:, cols].bitcast(FP8X4),
+                lhsT_scale=scales_t[n + 1][:, cols],
+                rhs=codes_t[0][:, cols].bitcast(FP8X4),
+                rhs_scale=scales_t[0][:, cols],
                 start=start,
                 stop=stop,
             )
 
-        def finish(it, l_codes, l_scales):
-            stat = ps_s.tile([P, 3 * P], F32, name="stat")
-            total = stat[:, 0:P]
+        def m1(n):
+            stat_t[n] = ps_s.tile([P, 3 * P], F32, name="stat")
             for c in range(CM):
-                mx(total, l_codes, l_scales, c, c == 0, c == CM - 1)
-            mu = small.tile([P, P], F32, name="mu")
-            nc.scalar.mul(out=mu[:], in_=total, mul=1.0 / CM)
-            d = work.tile([P, CM * P], F32, name="d")
-            sq = work.tile([P, CM * P], F32, name="sq")
-            for b in range(4):
-                t_bank = ps_t.tile([P, 4 * P], F32, name="t_bank")
-                for cc in range(4):
-                    mx(t_bank[:, cc * P:(cc + 1) * P], l_codes, l_scales, 4 * b + cc, True, True)
-                cols = slice(b * 4 * P, (b + 1) * 4 * P)
-                nc.vector.tensor_tensor(
-                    out=d[:, cols].rearrange("p (c j) -> p c j", c=4),
-                    in0=t_bank[:].rearrange("p (c j) -> p c j", c=4),
-                    in1=mu[:].unsqueeze(1).to_broadcast([P, 4, P]),
-                    op=ALU.subtract,
-                )
-                nc.scalar.activation(out=sq[:, cols], in_=d[:, cols], func=ACT.Square)
-            for c in range(CM):
+                mx(stat_t[n][:, 0:P], n, c, c == 0, c == CM - 1)
+
+        def t_mx(n, b):
+            tb_t[(n, b)] = ps_t.tile([P, 4 * P], F32, name="t_bank")
+            for cc in range(4):
+                mx(tb_t[(n, b)][:, cc * P:(cc + 1) * P], n, 4 * b + cc, True, True)
+
+        def mean(n):
+            sb[("mu", n)] = small.tile([P, P], F32, name="mu")
+            nc.scalar.mul(out=sb[("mu", n)][:], in_=stat_t[n][:, 0:P], mul=1.0 / CM)
+
+        def centre(n, b):
+            if b == 0:
+                sb[("d", n)] = work.tile([P, CM * P], F32, name="d")
+            cols = slice(b * 4 * P, (b + 1) * 4 * P)
+            nc.vector.tensor_tensor(
+                out=sb[("d", n)][:, cols].rearrange("p (c j) -> p c j", c=4),
+                in0=tb_t[(n, b)][:].rearrange("p (c j) -> p c j", c=4),
+                in1=sb[("mu", n)][:].unsqueeze(1).to_broadcast([P, 4, P]),
+                op=ALU.subtract,
+            )
+
+        def square(n, b):
+            if b == 0:
+                sb[("sq", n)] = work.tile([P, CM * P], F32, name="sq")
+            cols = slice(b * 4 * P, (b + 1) * 4 * P)
+            nc.scalar.activation(out=sb[("sq", n)][:, cols], in_=sb[("d", n)][:, cols], func=ACT.Square)
+
+        def acc(n, b):
+            for c in range(4 * b, 4 * b + 4):
                 nc.tensor.matmul(
-                    out=stat[:, P:2 * P], lhsT=sq[:, c * P:(c + 1) * P], rhs=ident[:],
+                    out=stat_t[n][:, P:2 * P], lhsT=sb[("sq", n)][:, c * P:(c + 1) * P], rhs=ident[:],
                     start=(c == 0), stop=(c == CM - 1), is_transpose=True)
-            s2t = small.tile([P, P], F32, name="s2t")
-            nc.scalar.copy(out=s2t[:], in_=stat[:, P:2 * P])
-            nc.tensor.transpose(stat[:, 2 * P:3 * P], s2t[:], ident[:])
-            std = small.tile([P, P], F32, name="std")
+
+        def cp(n):
+            sb[("s2t", n)] = small.tile([P, P], F32, name="s2t")
+            nc.scalar.copy(out=sb[("s2t", n)][:], in_=stat_t[n][:, P:2 * P])
+
+        def bk(n):
+            nc.tensor.transpose(stat_t[n][:, 2 * P:3 * P], sb[("s2t", n)][:], ident[:])
+
+        def rt(n):
+            sb[("std", n)] = small.tile([P, P], F32, name="std")
             nc.scalar.activation(
-                out=std[:], in_=stat[:, 2 * P:3 * P], func=ACT.Sqrt, bias=eps_t[:], scale=1.0 / CM)
+                out=sb[("std", n)][:], in_=stat_t[n][:, 2 * P:3 * P], func=ACT.Sqrt,
+                bias=eps_t[:], scale=1.0 / CM)
+
+        def scale_and_store(n):
             rstd = small.tile([P, P], F32, name="rstd")
-            nc.vector.reciprocal(out=rstd[:], in_=std[:])
+            nc.vector.reciprocal(out=rstd[:], in_=sb[("std", n)][:])
             e = work.tile([P, CM * P], F32, name="e")
             for c in range(CM):
                 cols = slice(c * P, (c + 1) * P)
                 nc.vector.scalar_tensor_tensor(
-                    out=e[:, cols], in0=d[:, cols], scalar=w32[:, c:c + 1], in1=rstd[:],
+                    out=e[:, cols], in0=sb[("d", n)][:, cols], scalar=w32[:, c:c + 1], in1=rstd[:],
                     op0=ALU.mult, op1=ALU.mult)
             o = work.tile([P, P * CM], F32, name="o")
             o_jc = o[:].rearrange("p (j c) -> p j c", c=CM)
             e_jc = e[:].rearrange("p (c j) -> p j c", c=CM)
-            fv = FINAL_V_COLS
-            if fv > 0:
-                nc.vector.tensor_tensor(
-                    out=o_jc[:, 0:fv], in0=e_jc[:, 0:fv],
-                    in1=b32[:].unsqueeze(1).to_broadcast([P, fv, CM]), op=ALU.add)
-            if fv < P:
-                nc.gpsimd.tensor_tensor(
-                    out=o_jc[:, fv:P], in0=e_jc[:, fv:P],
-                    in1=b32[:].unsqueeze(1).to_broadcast([P, P - fv, CM]), op=ALU.add)
-            nc.sync.dma_start(
-                out=out[it * P:(it + 1) * P].rearrange("i j c -> i (j c)"), in_=o[:])
+            step = P // 4
+            last = n == N_TILES - 1
+            dram = out[n * P:(n + 1) * P].rearrange("i j c -> i (j c)")
+            for piece in range(4):
+                js = slice(piece * step, (piece + 1) * step)
+                engine = nc.vector if (last and piece < 3) else nc.gpsimd
+                engine.tensor_tensor(
+                    out=o_jc[:, js], in0=e_jc[:, js],
+                    in1=b32[:].unsqueeze(1).to_broadcast([P, step, CM]), op=ALU.add)
+                if last and piece == 1:
+                    nc.sync.dma_start(out=dram[:, 0:P * CM // 2], in_=o[:, 0:P * CM // 2])
+            if last:
+                nc.sync.dma_start(out=dram[:, P * CM // 2:], in_=o[:, P * CM // 2:])
+            else:
+                nc.sync.dma_start(out=dram, in_=o[:])
 
-        def prepare(it):
-            l_codes = cpool.tile([P, CM * P], U32, name="l_codes", align_bytes=64)
-            l_scales = cpool.tile([P, CM * P], U8, name="l_scales", align_bytes=64)
-            quantise(left[it * P:(it + 1) * P], l_codes, l_scales, V_BANKS[it + 1])
-            return l_codes, l_scales
-
-        quantise(right, r_codes, r_scales, V_BANKS[0])
-        ready = prepare(0)
-        for it in range(N_TILES):
-            following = prepare(it + 1) if it + 1 < N_TILES else None
-            finish(it, ready[0], ready[1])
-            ready = following
+        for u in range(3):
+            load(u)
+        for u in range(2):
+            for b in range(BANKS):
+                tr(u, [b])
+                co(u, [b])
+        quant(0)
+        tr(2, [0, 1])
+        for k in range(N_TILES + 1):
+            u = k + 2
+            live = k < N_TILES
+            load(u + 1)
+            quant(k + 1)
+            co(u, [0])
+            if k >= 1:
+                rt(k - 1)
+            tr(u, [2, 3])
+            if live:
+                m1(k)
+                for b in range(3):
+                    t_mx(k, b)
+            if k >= 1:
+                scale_and_store(k - 1)
+            co(u, [1, 2, 3])
+            tr(u, [4, 5, 6, 7])
+            if live:
+                mean(k)
+            co(u, [4])
+            tr(u + 1, [0])
+            if live:
+                for b in range(4):
+                    centre(k, b)
+                    if b == 0:
+                        t_mx(k, 3)
+                    square(k, b)
+                    acc(k, b)
+            co(u, [5, 6, 7])
+            if live:
+                cp(k)
+            tr(u + 1, [1])
+            if live:
+                bk(k)

@@ -30,7 +30,7 @@ def tile_trianglemultiplication_pa_t_kernel(tc, left, right, ln_c_w, ln_c_b, out
     nc = tc.nc
     with ExitStack() as ctx:
         const = ctx.enter_context(tc.tile_pool(name="const", bufs=1))
-        xpool = ctx.enter_context(tc.tile_pool(name="xpool", bufs=12))
+        xpool = ctx.enter_context(tc.tile_pool(name="xpool", bufs=20))
         gpool = ctx.enter_context(tc.tile_pool(name="gpool", bufs=2))
         cpool = ctx.enter_context(tc.tile_pool(name="cpool", bufs=2))
         work = ctx.enter_context(tc.tile_pool(name="work", bufs=2))
@@ -211,7 +211,7 @@ def tile_trianglemultiplication_pa_t_kernel(tc, left, right, ln_c_w, ln_c_b, out
             else:
                 nc.sync.dma_start(out=dram, in_=o[:])
 
-        for u in range(3):
+        for u in range(5):
             load(u)
         for u in range(2):
             for b in range(BANKS):
@@ -222,7 +222,7 @@ def tile_trianglemultiplication_pa_t_kernel(tc, left, right, ln_c_w, ln_c_b, out
         for k in range(N_TILES + 1):
             u = k + 2
             live = k < N_TILES
-            load(u + 1)
+            load(u + 3)
             quant(k + 1)
             co(u, [0])
             if k >= 1:

@@ -105,21 +105,19 @@ def tile_trianglemultiplication_pa_t_kernel(tc, left, right, ln_c_w, ln_c_b, out
                 else:
                     nc.scalar.copy(out=dst, in_=src)
 
-        def quant(u):
+        def quant(u, h):
             if u >= N_UNITS:
                 return
-            pool = const if u == 0 else cpool
-            codes = pool.tile([P, CM * P], U32, name="codes" if u else "r_codes", align_bytes=64)
-            scales = pool.tile([P, CM * P], U8, name="scales" if u else "r_scales", align_bytes=64)
-            codes_t[u] = codes
-            scales_t[u] = scales
+            if h == 0:
+                pool = const if u == 0 else cpool
+                codes_t[u] = pool.tile([P, CM * P], U32, name="codes" if u else "r_codes", align_bytes=64)
+                scales_t[u] = pool.tile([P, CM * P], U8, name="scales" if u else "r_scales", align_bytes=64)
             half = ROW // 2
-            for h in range(2):
-                nc.vector.quantize_mx(
-                    out=codes[:, h * half // PACK:(h + 1) * half // PACK].bitcast(FP8X4),
-                    scales=scales[:, h * half // PACK:(h + 1) * half // PACK],
-                    in_=grouped_t[u][:, h * half:(h + 1) * half],
-                )
+            nc.vector.quantize_mx(
+                out=codes_t[u][:, h * half // PACK:(h + 1) * half // PACK].bitcast(FP8X4),
+                scales=scales_t[u][:, h * half // PACK:(h + 1) * half // PACK],
+                in_=grouped_t[u][:, h * half:(h + 1) * half],
+            )
 
         def mx(acc, n, c, start, stop):
             cols = slice(c * P, (c + 1) * P)
@@ -134,7 +132,7 @@ def tile_trianglemultiplication_pa_t_kernel(tc, left, right, ln_c_w, ln_c_b, out
             )
 
         def m1(n):
-            stat_t[n] = ps_s.tile([P, 3 * P], F32, name="stat")
+            stat_t[n] = ps_s.tile([P, 2 * P], F32, name="stat")
             for c in range(CM):
                 mx(stat_t[n][:, 0:P], n, c, c == 0, c == CM - 1)
 
@@ -170,46 +168,52 @@ def tile_trianglemultiplication_pa_t_kernel(tc, left, right, ln_c_w, ln_c_b, out
                     out=stat_t[n][:, P:2 * P], lhsT=sb[("sq", n)][:, c * P:(c + 1) * P], rhs=ident[:],
                     start=(c == 0), stop=(c == CM - 1), is_transpose=True)
 
-        def cp(n):
-            sb[("s2t", n)] = small.tile([P, P], F32, name="s2t")
-            nc.scalar.copy(out=sb[("s2t", n)][:], in_=stat_t[n][:, P:2 * P])
-
-        def bk(n):
-            nc.tensor.transpose(stat_t[n][:, 2 * P:3 * P], sb[("s2t", n)][:], ident[:])
-
         def rt(n):
             sb[("std", n)] = small.tile([P, P], F32, name="std")
             nc.scalar.activation(
-                out=sb[("std", n)][:], in_=stat_t[n][:, 2 * P:3 * P], func=ACT.Sqrt,
+                out=sb[("std", n)][:], in_=stat_t[n][:, P:2 * P], func=ACT.Sqrt,
                 bias=eps_t[:], scale=1.0 / CM)
 
+        def rc(n):
+            sb[("rstdT", n)] = small.tile([P, P], F32, name="rstdT")
+            nc.vector.reciprocal(out=sb[("rstdT", n)][:], in_=sb[("std", n)][:])
+
+        def bk(n):
+            sb[("rstd", n)] = ps_t.tile([P, 4 * P], F32, name="t_bank")
+            nc.tensor.transpose(sb[("rstd", n)][:, 0:P], sb[("rstdT", n)][:], ident[:])
+
         def scale_and_store(n):
-            rstd = small.tile([P, P], F32, name="rstd")
-            nc.vector.reciprocal(out=rstd[:], in_=sb[("std", n)][:])
+            rstd = sb[("rstd", n)][:, 0:P]
             e = work.tile([P, CM * P], F32, name="e")
-            for c in range(CM):
-                cols = slice(c * P, (c + 1) * P)
-                nc.vector.scalar_tensor_tensor(
-                    out=e[:, cols], in0=sb[("d", n)][:, cols], scalar=w32[:, c:c + 1], in1=rstd[:],
-                    op0=ALU.mult, op1=ALU.mult)
             o = work.tile([P, P * CM], F32, name="o")
             o_jc = o[:].rearrange("p (j c) -> p j c", c=CM)
             e_jc = e[:].rearrange("p (c j) -> p j c", c=CM)
-            step = P // 4
             last = n == N_TILES - 1
             dram = out[n * P:(n + 1) * P].rearrange("i j c -> i (j c)")
+            for b in range(4):
+                for c in range(4 * b, 4 * b + 4):
+                    cols = slice(c * P, (c + 1) * P)
+                    nc.vector.scalar_tensor_tensor(
+                        out=e[:, cols], in0=sb[("d", n)][:, cols], scalar=w32[:, c:c + 1], in1=rstd,
+                        op0=ALU.mult, op1=ALU.mult)
+                if not last:
+                    cs = slice(4 * b, 4 * b + 4)
+                    nc.gpsimd.tensor_tensor(
+                        out=o_jc[:, :, cs], in0=e_jc[:, :, cs],
+                        in1=b32[:, cs].unsqueeze(1).to_broadcast([P, P, 4]), op=ALU.add)
+            if not last:
+                nc.sync.dma_start(out=dram, in_=o[:])
+                return
+            step = P // 4
             for piece in range(4):
                 js = slice(piece * step, (piece + 1) * step)
-                engine = nc.vector if (last and piece < 3) else nc.gpsimd
+                engine = nc.vector if piece < 3 else nc.gpsimd
                 engine.tensor_tensor(
                     out=o_jc[:, js], in0=e_jc[:, js],
                     in1=b32[:].unsqueeze(1).to_broadcast([P, step, CM]), op=ALU.add)
-                if last and piece == 1:
+                if piece == 1:
                     nc.sync.dma_start(out=dram[:, 0:P * CM // 2], in_=o[:, 0:P * CM // 2])
-            if last:
-                nc.sync.dma_start(out=dram[:, P * CM // 2:], in_=o[:, P * CM // 2:])
-            else:
-                nc.sync.dma_start(out=dram, in_=o[:])
+            nc.sync.dma_start(out=dram[:, P * CM // 2:], in_=o[:, P * CM // 2:])
 
         for u in range(5):
             load(u)
@@ -217,39 +221,47 @@ def tile_trianglemultiplication_pa_t_kernel(tc, left, right, ln_c_w, ln_c_b, out
             for b in range(BANKS):
                 tr(u, [b])
                 co(u, [b])
-        quant(0)
+        quant(0, 0)
+        quant(0, 1)
         tr(2, [0, 1])
         for k in range(N_TILES + 1):
             u = k + 2
             live = k < N_TILES
             load(u + 3)
-            quant(k + 1)
-            co(u, [0])
+            quant(k + 1, 0)
             if k >= 1:
-                rt(k - 1)
+                rc(k - 1)
+            quant(k + 1, 1)
+            co(u, [0])
             tr(u, [2, 3])
+            if k >= 1:
+                bk(k - 1)
             if live:
                 m1(k)
-                for b in range(3):
+                for b in range(2):
                     t_mx(k, b)
             if k >= 1:
                 scale_and_store(k - 1)
-            co(u, [1, 2, 3])
-            tr(u, [4, 5, 6, 7])
+            co(u, [1, 2])
             if live:
                 mean(k)
+            co(u, [3])
+            tr(u, [4, 5])
+            if live:
+                t_mx(k, 2)
+                centre(k, 0)
+                t_mx(k, 3)
+            tr(u, [6, 7])
             co(u, [4])
             tr(u + 1, [0])
             if live:
-                for b in range(4):
+                square(k, 0)
+                acc(k, 0)
+                for b in range(1, 4):
                     centre(k, b)
-                    if b == 0:
-                        t_mx(k, 3)
                     square(k, b)
                     acc(k, b)
             co(u, [5, 6, 7])
             if live:
-                cp(k)
+                rt(k)
             tr(u + 1, [1])
-            if live:
-                bk(k)

@@ -31,7 +31,7 @@ def tile_trianglemultiplication_pa_t_kernel(tc, left, right, ln_c_w, ln_c_b, out
     with ExitStack() as ctx:
         const = ctx.enter_context(tc.tile_pool(name="const", bufs=1))
         xpool = ctx.enter_context(tc.tile_pool(name="xpool", bufs=20))
-        gpool = ctx.enter_context(tc.tile_pool(name="gpool", bufs=2))
+        gpool = ctx.enter_context(tc.tile_pool(name="gpool", bufs=3))
         cpool = ctx.enter_context(tc.tile_pool(name="cpool", bufs=2))
         work = ctx.enter_context(tc.tile_pool(name="work", bufs=2))
         small = ctx.enter_context(tc.tile_pool(name="small", bufs=2))
@@ -42,8 +42,6 @@ def tile_trianglemultiplication_pa_t_kernel(tc, left, right, ln_c_w, ln_c_b, out
 
         w16 = const.tile([P, CM], BF16)
         b16 = const.tile([P, CM], BF16)
-        nc.scalar.dma_start(out=w16[:], in_=ln_c_w.partition_broadcast(P))
-        nc.scalar.dma_start(out=b16[:], in_=ln_c_b.partition_broadcast(P))
         eps_t = const.tile([P, 1], F32)
         nc.vector.memset(eps_t[:], EPS)
         warm = const.tile([P, 1], F32)
@@ -52,8 +50,6 @@ def tile_trianglemultiplication_pa_t_kernel(tc, left, right, ln_c_w, ln_c_b, out
         make_identity(nc, ident[:])
         w32 = const.tile([P, CM], F32)
         b32 = const.tile([P, CM], F32)
-        nc.vector.tensor_copy(out=w32[:], in_=w16[:])
-        nc.vector.tensor_copy(out=b32[:], in_=b16[:])
 
         x_t = {}
         bank_t = {}
@@ -99,7 +95,7 @@ def tile_trianglemultiplication_pa_t_kernel(tc, left, right, ln_c_w, ln_c_b, out
                 src = bank_t[(u, b)][:].bitcast(BF16).rearrange("p (q r e) -> p q e r", q=4, e=2)
                 dst = by_channel[:, 8 * hb:8 * hb + 8, g * P:(g + 1) * P].rearrange(
                     "p (q e) r -> p q e r", e=2)
-                on_vector = (b % 2 == 1) if u < 2 else (b in (5, 7))
+                on_vector = (b % 2 == 1) if u == 0 else (b in (3, 5, 7)) if u == 1 else (b in (5, 7))
                 if on_vector:
                     nc.vector.tensor_copy(out=dst, in_=src)
                 else:
@@ -217,12 +213,16 @@ def tile_trianglemultiplication_pa_t_kernel(tc, left, right, ln_c_w, ln_c_b, out
 
         for u in range(5):
             load(u)
-        for u in range(2):
-            for b in range(BANKS):
-                tr(u, [b])
-                co(u, [b])
+        for b in range(BANKS):
+            tr(0, [b])
+            co(0, [b])
+        nc.scalar.dma_start(out=w16[:], in_=ln_c_w.partition_broadcast(P))
+        nc.scalar.dma_start(out=b16[:], in_=ln_c_b.partition_broadcast(P))
         quant(0, 0)
         quant(0, 1)
+        for b in range(BANKS):
+            tr(1, [b])
+            co(1, [b])
         tr(2, [0, 1])
         for k in range(N_TILES + 1):
             u = k + 2
@@ -232,6 +232,9 @@ def tile_trianglemultiplication_pa_t_kernel(tc, left, right, ln_c_w, ln_c_b, out
             if k >= 1:
                 rc(k - 1)
             quant(k + 1, 1)
+            if k == 1:
+                nc.vector.tensor_copy(out=w32[:], in_=w16[:])
+                nc.vector.tensor_copy(out=b32[:], in_=b16[:])
             co(u, [0])
             tr(u, [2, 3])
             if k >= 1:

@@ -133,7 +133,10 @@ def tile_trianglemultiplication_pa_t_kernel(tc, left, right, ln_c_w, ln_c_b, out
                 mx(stat_t[n][:, 0:P], n, c, c == 0, c == CM - 1)
 
         def t_mx(n, b):
-            tb_t[(n, b)] = ps_t.tile([P, 4 * P], F32, name="t_bank")
+            if n == N_TILES - 1:
+                tb_t[(n, b)] = ps_tr.tile([P, 4 * P], F32, name="bank")
+            else:
+                tb_t[(n, b)] = ps_t.tile([P, 4 * P], F32, name="t_bank")
             for cc in range(4):
                 mx(tb_t[(n, b)][:, cc * P:(cc + 1) * P], n, 4 * b + cc, True, True)
 
@@ -178,38 +181,47 @@ def tile_trianglemultiplication_pa_t_kernel(tc, left, right, ln_c_w, ln_c_b, out
             sb[("rstd", n)] = ps_t.tile([P, 4 * P], F32, name="t_bank")
             nc.tensor.transpose(sb[("rstd", n)][:, 0:P], sb[("rstdT", n)][:], ident[:])
 
-        def scale_and_store(n):
+        def scale(n, b):
+            if b == 0:
+                sb[("e", n)] = work.tile([P, CM * P], F32, name="e")
+                sb[("o", n)] = work.tile([P, P * CM], F32, name="o")
             rstd = sb[("rstd", n)][:, 0:P]
-            e = work.tile([P, CM * P], F32, name="e")
-            o = work.tile([P, P * CM], F32, name="o")
-            o_jc = o[:].rearrange("p (j c) -> p j c", c=CM)
-            e_jc = e[:].rearrange("p (c j) -> p j c", c=CM)
-            last = n == N_TILES - 1
-            dram = out[n * P:(n + 1) * P].rearrange("i j c -> i (j c)")
+            e = sb[("e", n)]
+            for c in range(4 * b, 4 * b + 4):
+                cols = slice(c * P, (c + 1) * P)
+                nc.vector.scalar_tensor_tensor(
+                    out=e[:, cols], in0=sb[("d", n)][:, cols], scalar=w32[:, c:c + 1], in1=rstd,
+                    op0=ALU.mult, op1=ALU.mult)
+
+        def add_group(n, b, engine):
+            cs = slice(4 * b, 4 * b + 4)
+            engine.tensor_tensor(
+                out=sb[("o", n)][:].rearrange("p (j c) -> p j c", c=CM)[:, :, cs],
+                in0=sb[("e", n)][:].rearrange("p (c j) -> p j c", c=CM)[:, :, cs],
+                in1=b32[:, cs].unsqueeze(1).to_broadcast([P, P, 4]), op=ALU.add)
+
+        def store(n):
+            nc.sync.dma_start(out=out[n * P:(n + 1) * P].rearrange("i j c -> i (j c)"), in_=sb[("o", n)][:])
+
+        def scale_and_store(n):
             for b in range(4):
-                for c in range(4 * b, 4 * b + 4):
-                    cols = slice(c * P, (c + 1) * P)
-                    nc.vector.scalar_tensor_tensor(
-                        out=e[:, cols], in0=sb[("d", n)][:, cols], scalar=w32[:, c:c + 1], in1=rstd,
-                        op0=ALU.mult, op1=ALU.mult)
-                if not last:
-                    cs = slice(4 * b, 4 * b + 4)
-                    nc.gpsimd.tensor_tensor(
-                        out=o_jc[:, :, cs], in0=e_jc[:, :, cs],
-                        in1=b32[:, cs].unsqueeze(1).to_broadcast([P, P, 4]), op=ALU.add)
-            if not last:
-                nc.sync.dma_start(out=dram, in_=o[:])
-                return
+                scale(n, b)
+                add_group(n, b, nc.gpsimd)
+            store(n)
+
+        def last_add_and_store(n):
+            o_jc = sb[("o", n)][:].rearrange("p (j c) -> p j c", c=CM)
+            e_jc = sb[("e", n)][:].rearrange("p (c j) -> p j c", c=CM)
+            dram = out[n * P:(n + 1) * P].rearrange("i j c -> i (j c)")
             step = P // 4
             for piece in range(4):
                 js = slice(piece * step, (piece + 1) * step)
-                engine = nc.vector if piece < 3 else nc.gpsimd
-                engine.tensor_tensor(
+                nc.vector.tensor_tensor(
                     out=o_jc[:, js], in0=e_jc[:, js],
                     in1=b32[:].unsqueeze(1).to_broadcast([P, step, CM]), op=ALU.add)
                 if piece == 1:
-                    nc.sync.dma_start(out=dram[:, 0:P * CM // 2], in_=o[:, 0:P * CM // 2])
-            nc.sync.dma_start(out=dram[:, P * CM // 2:], in_=o[:, P * CM // 2:])
+                    nc.sync.dma_start(out=dram[:, 0:P * CM // 2], in_=sb[("o", n)][:, 0:P * CM // 2])
+            nc.sync.dma_start(out=dram[:, P * CM // 2:], in_=sb[("o", n)][:, P * CM // 2:])
 
         for u in range(5):
             load(u)
@@ -224,9 +236,8 @@ def tile_trianglemultiplication_pa_t_kernel(tc, left, right, ln_c_w, ln_c_b, out
             tr(1, [b])
             co(1, [b])
         tr(2, [0, 1])
-        for k in range(N_TILES + 1):
+        for k in range(N_TILES - 1):
             u = k + 2
-            live = k < N_TILES
             load(u + 3)
             quant(k + 1, 0)
             if k >= 1:
@@ -239,32 +250,55 @@ def tile_trianglemultiplication_pa_t_kernel(tc, left, right, ln_c_w, ln_c_b, out
             tr(u, [2, 3])
             if k >= 1:
                 bk(k - 1)
-            if live:
-                m1(k)
-                for b in range(2):
-                    t_mx(k, b)
+            m1(k)
+            for b in range(2):
+                t_mx(k, b)
             if k >= 1:
                 scale_and_store(k - 1)
             co(u, [1, 2])
-            if live:
-                mean(k)
+            mean(k)
             co(u, [3])
             tr(u, [4, 5])
-            if live:
-                t_mx(k, 2)
-                centre(k, 0)
-                t_mx(k, 3)
+            t_mx(k, 2)
+            centre(k, 0)
+            t_mx(k, 3)
             tr(u, [6, 7])
             co(u, [4])
             tr(u + 1, [0])
-            if live:
-                square(k, 0)
-                acc(k, 0)
-                for b in range(1, 4):
-                    centre(k, b)
-                    square(k, b)
-                    acc(k, b)
+            square(k, 0)
+            acc(k, 0)
+            for b in range(1, 4):
+                centre(k, b)
+                square(k, b)
+                acc(k, b)
             co(u, [5, 6, 7])
-            if live:
-                rt(k)
+            rt(k)
             tr(u + 1, [1])
+
+        n = N_TILES - 1
+        quant(n + 1, 0)
+        rc(n - 1)
+        quant(n + 1, 1)
+        bk(n - 1)
+        m1(n)
+        for b in range(4):
+            t_mx(n, b)
+        for b in range(2):
+            scale(n - 1, b)
+            add_group(n - 1, b, nc.gpsimd)
+        mean(n)
+        for b in range(4):
+            centre(n, b)
+            square(n, b)
+            acc(n, b)
+        rt(n)
+        for b in range(2, 4):
+            scale(n - 1, b)
+        add_group(n - 1, 2, nc.vector)
+        rc(n)
+        bk(n)
+        add_group(n - 1, 3, nc.vector)
+        store(n - 1)
+        for b in range(4):
+            scale(n, b)
+        last_add_and_store(n)

@@ -45,7 +45,7 @@ def tile_trianglemultiplication_pa_t_kernel(tc, left, right, ln_c_w, ln_c_b, out
         eps_t = const.tile([P, 1], F32)
         nc.vector.memset(eps_t[:], EPS)
         warm = const.tile([P, 1], F32)
-        nc.scalar.activation(out=warm[:], in_=eps_t[:], func=ACT.Sqrt)
+        nc.scalar.activation(out=warm[:], in_=eps_t[:], func=ACT.Abs_reciprocal_sqrt)
         ident = const.tile([P, P], F32)
         make_identity(nc, ident[:])
         w32 = const.tile([P, CM], F32)
@@ -168,14 +168,10 @@ def tile_trianglemultiplication_pa_t_kernel(tc, left, right, ln_c_w, ln_c_b, out
                     start=(c == 0), stop=(c == CM - 1), is_transpose=True)
 
         def rt(n):
-            sb[("std", n)] = small.tile([P, P], F32, name="std")
-            nc.scalar.activation(
-                out=sb[("std", n)][:], in_=stat_t[n][:, P:2 * P], func=ACT.Sqrt,
-                bias=eps_t[:], scale=1.0 / CM)
-
-        def rc(n):
             sb[("rstdT", n)] = small.tile([P, P], F32, name="rstdT")
-            nc.vector.reciprocal(out=sb[("rstdT", n)][:], in_=sb[("std", n)][:])
+            nc.scalar.activation(
+                out=sb[("rstdT", n)][:], in_=stat_t[n][:, P:2 * P], func=ACT.Abs_reciprocal_sqrt,
+                bias=eps_t[:], scale=1.0 / CM)
 
         def bk(n):
             sb[("rstd", n)] = ps_t.tile([P, 4 * P], F32, name="t_bank")
@@ -240,8 +236,6 @@ def tile_trianglemultiplication_pa_t_kernel(tc, left, right, ln_c_w, ln_c_b, out
             u = k + 2
             load(u + 3)
             quant(k + 1, 0)
-            if k >= 1:
-                rc(k - 1)
             quant(k + 1, 1)
             if k == 1:
                 nc.vector.tensor_copy(out=w32[:], in_=w16[:])
@@ -277,7 +271,6 @@ def tile_trianglemultiplication_pa_t_kernel(tc, left, right, ln_c_w, ln_c_b, out
 
         n = N_TILES - 1
         quant(n + 1, 0)
-        rc(n - 1)
         quant(n + 1, 1)
         bk(n - 1)
         m1(n)
@@ -295,7 +288,6 @@ def tile_trianglemultiplication_pa_t_kernel(tc, left, right, ln_c_w, ln_c_b, out
         for b in range(2, 4):
             scale(n - 1, b)
         add_group(n - 1, 2, nc.vector)
-        rc(n)
         bk(n)
         add_group(n - 1, 3, nc.vector)
         store(n - 1)

@@ -30,10 +30,11 @@ def tile_trianglemultiplication_pa_t_kernel(tc, left, right, ln_c_w, ln_c_b, out
     nc = tc.nc
     with ExitStack() as ctx:
         const = ctx.enter_context(tc.tile_pool(name="const", bufs=1))
-        xpool = ctx.enter_context(tc.tile_pool(name="xpool", bufs=20))
+        xpool = ctx.enter_context(tc.tile_pool(name="xpool", bufs=16))
         gpool = ctx.enter_context(tc.tile_pool(name="gpool", bufs=3))
-        cpool = ctx.enter_context(tc.tile_pool(name="cpool", bufs=2))
+        cpool = ctx.enter_context(tc.tile_pool(name="cpool", bufs=3))
         work = ctx.enter_context(tc.tile_pool(name="work", bufs=2))
+        opool = ctx.enter_context(tc.tile_pool(name="opool", bufs=3))
         small = ctx.enter_context(tc.tile_pool(name="small", bufs=2))
         ps_tr = ctx.enter_context(tc.psum_pool(name="ps_tr", bufs=4))
         ps_t = ctx.enter_context(tc.psum_pool(name="ps_t", bufs=3))
@@ -49,7 +50,9 @@ def tile_trianglemultiplication_pa_t_kernel(tc, left, right, ln_c_w, ln_c_b, out
         ident = const.tile([P, P], F32)
         make_identity(nc, ident[:])
         w32 = const.tile([P, CM], F32)
-        b32 = const.tile([P, CM], F32)
+        b_pad = const.tile([P, P], F32)
+        nc.gpsimd.memset(b_pad[:], 0.0)
+        b32 = b_pad[:, 0:CM]
 
         x_t = {}
         bank_t = {}
@@ -95,7 +98,7 @@ def tile_trianglemultiplication_pa_t_kernel(tc, left, right, ln_c_w, ln_c_b, out
                 src = bank_t[(u, b)][:].bitcast(BF16).rearrange("p (q r e) -> p q e r", q=4, e=2)
                 dst = by_channel[:, 8 * hb:8 * hb + 8, g * P:(g + 1) * P].rearrange(
                     "p (q e) r -> p q e r", e=2)
-                on_vector = (b % 2 == 1) if u == 0 else (b in (3, 5, 7)) if u == 1 else (b in (5, 7))
+                on_vector = (b % 2 == 1) if u == 0 else (b in (3, 5, 7)) if u <= 2 else (b in (5, 7))
                 if on_vector:
                     nc.vector.tensor_copy(out=dst, in_=src)
                 else:
@@ -128,12 +131,15 @@ def tile_trianglemultiplication_pa_t_kernel(tc, left, right, ln_c_w, ln_c_b, out
             )
 
         def m1(n):
-            stat_t[n] = ps_s.tile([P, 2 * P], F32, name="stat")
+            if n == N_TILES - 1:
+                stat_t[n] = ps_t.tile([P, 4 * P], F32, name="t_bank")
+            else:
+                stat_t[n] = ps_s.tile([P, 2 * P], F32, name="stat")
             for c in range(CM):
                 mx(stat_t[n][:, 0:P], n, c, c == 0, c == CM - 1)
 
         def t_mx(n, b):
-            if n == N_TILES - 1:
+            if n >= N_TILES - 2:
                 tb_t[(n, b)] = ps_tr.tile([P, 4 * P], F32, name="bank")
             else:
                 tb_t[(n, b)] = ps_t.tile([P, 4 * P], F32, name="t_bank")
@@ -174,13 +180,16 @@ def tile_trianglemultiplication_pa_t_kernel(tc, left, right, ln_c_w, ln_c_b, out
                 bias=eps_t[:], scale=1.0 / CM)
 
         def bk(n):
-            sb[("rstd", n)] = ps_t.tile([P, 4 * P], F32, name="t_bank")
+            if n == N_TILES - 1:
+                sb[("rstd", n)] = sb[("rstd", n - 1)][:, P:3 * P]
+            else:
+                sb[("rstd", n)] = ps_t.tile([P, 4 * P], F32, name="t_bank")
             nc.tensor.transpose(sb[("rstd", n)][:, 0:P], sb[("rstdT", n)][:], ident[:])
 
         def scale(n, b):
             if b == 0:
                 sb[("e", n)] = work.tile([P, CM * P], F32, name="e")
-                sb[("o", n)] = work.tile([P, P * CM], F32, name="o")
+                sb[("o", n)] = opool.tile([P, P * CM], F32, name="o")
             rstd = sb[("rstd", n)][:, 0:P]
             e = sb[("e", n)]
             for c in range(4 * b, 4 * b + 4):
@@ -189,12 +198,12 @@ def tile_trianglemultiplication_pa_t_kernel(tc, left, right, ln_c_w, ln_c_b, out
                     out=e[:, cols], in0=sb[("d", n)][:, cols], scalar=w32[:, c:c + 1], in1=rstd,
                     op0=ALU.mult, op1=ALU.mult)
 
-        def add_group(n, b, engine):
+        def add_group(n, b, engine, bias):
             cs = slice(4 * b, 4 * b + 4)
             engine.tensor_tensor(
                 out=sb[("o", n)][:].rearrange("p (j c) -> p j c", c=CM)[:, :, cs],
                 in0=sb[("e", n)][:].rearrange("p (c j) -> p j c", c=CM)[:, :, cs],
-                in1=b32[:, cs].unsqueeze(1).to_broadcast([P, P, 4]), op=ALU.add)
+                in1=bias[:, cs].unsqueeze(1).to_broadcast([P, P, 4]), op=ALU.add)
 
         def store(n):
             nc.sync.dma_start(out=out[n * P:(n + 1) * P].rearrange("i j c -> i (j c)"), in_=sb[("o", n)][:])
@@ -202,28 +211,34 @@ def tile_trianglemultiplication_pa_t_kernel(tc, left, right, ln_c_w, ln_c_b, out
         def scale_and_store(n):
             for b in range(4):
                 scale(n, b)
-                add_group(n, b, nc.gpsimd)
+                add_group(n, b, nc.gpsimd, b32)
             store(n)
 
-        def last_add_and_store(n):
+        def last_add_and_store(n, b_ps):
             o_jc = sb[("o", n)][:].rearrange("p (j c) -> p j c", c=CM)
             e_jc = sb[("e", n)][:].rearrange("p (c j) -> p j c", c=CM)
             dram = out[n * P:(n + 1) * P].rearrange("i j c -> i (j c)")
             step = P // 4
+            nc.gpsimd.tensor_tensor(
+                out=o_jc[:, 3 * step:], in0=e_jc[:, 3 * step:],
+                in1=b32.unsqueeze(1).to_broadcast([P, step, CM]), op=ALU.add)
             for piece in range(4):
                 js = slice(piece * step, (piece + 1) * step)
+                if piece == 3:
+                    continue
                 nc.vector.tensor_tensor(
                     out=o_jc[:, js], in0=e_jc[:, js],
-                    in1=b32[:].unsqueeze(1).to_broadcast([P, step, CM]), op=ALU.add)
+                    in1=b_ps.unsqueeze(1).to_broadcast([P, step, CM]), op=ALU.add)
                 if piece == 1:
                     nc.sync.dma_start(out=dram[:, 0:P * CM // 2], in_=sb[("o", n)][:, 0:P * CM // 2])
             nc.sync.dma_start(out=dram[:, P * CM // 2:], in_=sb[("o", n)][:, P * CM // 2:])
 
-        for u in range(5):
+        for u in range(4):
             load(u)
         for b in range(BANKS):
             tr(0, [b])
             co(0, [b])
+        load(4)
         nc.scalar.dma_start(out=w16[:], in_=ln_c_w.partition_broadcast(P))
         nc.scalar.dma_start(out=b16[:], in_=ln_c_b.partition_broadcast(P))
         quant(0, 0)
@@ -231,15 +246,21 @@ def tile_trianglemultiplication_pa_t_kernel(tc, left, right, ln_c_w, ln_c_b, out
         for b in range(BANKS):
             tr(1, [b])
             co(1, [b])
-        tr(2, [0, 1])
-        for k in range(N_TILES - 1):
-            u = k + 2
+        load(5)
+        quant(1, 0)
+        quant(1, 1)
+        for b in range(BANKS):
+            tr(2, [b])
+            co(2, [b])
+        tr(3, [0, 1])
+        for k in range(N_TILES - 2):
+            u = k + 3
             load(u + 3)
-            quant(k + 1, 0)
-            quant(k + 1, 1)
+            quant(k + 2, 0)
+            quant(k + 2, 1)
             if k == 1:
                 nc.vector.tensor_copy(out=w32[:], in_=w16[:])
-                nc.vector.tensor_copy(out=b32[:], in_=b16[:])
+                nc.vector.tensor_copy(out=b32, in_=b16[:])
             co(u, [0])
             tr(u, [2, 3])
             if k >= 1:
@@ -272,25 +293,43 @@ def tile_trianglemultiplication_pa_t_kernel(tc, left, right, ln_c_w, ln_c_b, out
         n = N_TILES - 1
         quant(n + 1, 0)
         quant(n + 1, 1)
-        bk(n - 1)
+        turned = ps_tr.tile([P, 4 * P], F32, name="bank")
+        nc.tensor.transpose(turned[:, 0:P], b_pad[:], ident[:])
+        b_rows = small.tile([P, P], F32, name="b_rows")
+        nc.scalar.copy(out=b_rows[:], in_=turned[:, 0:P])
+        bk(n - 2)
+        m1(n - 1)
+        for b in range(4):
+            t_mx(n - 1, b)
+        b_bank = ps_t.tile([P, 4 * P], F32, name="t_bank")
+        nc.tensor.transpose(b_bank[:, 0:P], b_rows[:], ident[:])
+        b_ps = b_bank[:, 0:CM]
+        mean(n - 1)
         m1(n)
         for b in range(4):
+            centre(n - 1, b)
+            square(n - 1, b)
             t_mx(n, b)
-        for b in range(2):
-            scale(n - 1, b)
-            add_group(n - 1, b, nc.gpsimd)
         mean(n)
+        for b in range(4):
+            acc(n - 1, b)
+        rt(n - 1)
+        scale_and_store(n - 2)
         for b in range(4):
             centre(n, b)
             square(n, b)
+        bk(n - 1)
+        for b in range(4):
             acc(n, b)
         rt(n)
-        for b in range(2, 4):
+        for b in range(4):
             scale(n - 1, b)
-        add_group(n - 1, 2, nc.vector)
-        bk(n)
-        add_group(n - 1, 3, nc.vector)
+            if b < 2:
+                add_group(n - 1, b, nc.gpsimd, b32)
+        for b in range(2, 4):
+            add_group(n - 1, b, nc.vector, b_ps)
         store(n - 1)
+        bk(n)
         for b in range(4):
             scale(n, b)
-        last_add_and_store(n)
+        last_add_and_store(n, b_ps)

@@ -81,7 +81,10 @@ def tile_trianglemultiplication_pa_t_kernel(tc, left, right, ln_c_w, ln_c_b, out
             for b in banks:
                 g, hb = b // 2, b % 2
                 words = x_t[(u, g)][:].bitcast(F32).rearrange("r (p q) -> r q p", q=CPAIRS)
-                bank = ps_tr.tile([P, 4 * P], F32, name="bank")
+                if u < 3 and b % 2 == 1:
+                    bank = ps_t.tile([P, 4 * P], F32, name="t_bank")
+                else:
+                    bank = ps_tr.tile([P, 4 * P], F32, name="bank")
                 for ql in range(4):
                     nc.tensor.transpose(
                         bank[:, ql * P:(ql + 1) * P], words[:, 4 * hb + ql, :], ident[:])

@@ -201,20 +201,22 @@ def tile_trianglemultiplication_pa_t_kernel(tc, left, right, ln_c_w, ln_c_b, out
                     out=e[:, cols], in0=sb[("d", n)][:, cols], scalar=w32[:, c:c + 1], in1=rstd,
                     op0=ALU.mult, op1=ALU.mult)
 
-        def add_group(n, b, engine, bias):
-            cs = slice(4 * b, 4 * b + 4)
+        def add_groups(n, lo, hi, engine, bias):
             engine.tensor_tensor(
-                out=sb[("o", n)][:].rearrange("p (j c) -> p j c", c=CM)[:, :, cs],
-                in0=sb[("e", n)][:].rearrange("p (c j) -> p j c", c=CM)[:, :, cs],
-                in1=bias[:, cs].unsqueeze(1).to_broadcast([P, P, 4]), op=ALU.add)
+                out=sb[("o", n)][:].rearrange("p (j g c) -> p g j c", g=4, c=4)[:, lo:hi],
+                in0=sb[("e", n)][:].rearrange("p (g c j) -> p g j c", g=4, c=4)[:, lo:hi],
+                in1=bias.rearrange("p (g c) -> p g c", g=4)[:, lo:hi].unsqueeze(2).to_broadcast(
+                    [P, hi - lo, P, 4]), op=ALU.add)
 
         def store(n):
             nc.sync.dma_start(out=out[n * P:(n + 1) * P].rearrange("i j c -> i (j c)"), in_=sb[("o", n)][:])
 
         def scale_and_store(n):
-            for b in range(4):
+            scale(n, 0)
+            add_groups(n, 0, 1, nc.gpsimd, b32)
+            for b in range(1, 4):
                 scale(n, b)
-                add_group(n, b, nc.gpsimd, b32)
+            add_groups(n, 1, 4, nc.gpsimd, b32)
             store(n)
 
         def last_add_and_store(n, b_ps):
@@ -328,9 +330,9 @@ def tile_trianglemultiplication_pa_t_kernel(tc, left, right, ln_c_w, ln_c_b, out
         for b in range(4):
             scale(n - 1, b)
             if b < 2:
-                add_group(n - 1, b, nc.gpsimd, b32)
+                add_groups(n - 1, b, b + 1, nc.gpsimd, b32)
         for b in range(2, 4):
-            add_group(n - 1, b, nc.vector, b_ps)
+            add_groups(n - 1, b, b + 1, nc.vector, b_ps)
         store(n - 1)
         bk(n)
         for b in range(4):

@@ -190,7 +190,7 @@ def tile_trianglemultiplication_pa_t_kernel(tc, left, right, ln_c_w, ln_c_b, out
             nc.tensor.transpose(sb[("rstd", n)][:, 0:P], sb[("rstdT", n)][:], ident[:])
 
         def scale(n, b):
-            if b == 0:
+            if ("e", n) not in sb:
                 sb[("e", n)] = work.tile([P, CM * P], F32, name="e")
                 sb[("o", n)] = opool.tile([P, P * CM], F32, name="o")
             rstd = sb[("rstd", n)][:, 0:P]
@@ -211,12 +211,40 @@ def tile_trianglemultiplication_pa_t_kernel(tc, left, right, ln_c_w, ln_c_b, out
         def store(n):
             nc.sync.dma_start(out=out[n * P:(n + 1) * P].rearrange("i j c -> i (j c)"), in_=sb[("o", n)][:])
 
+        def scale_by_rstd(n, b):
+            if ("e", n) not in sb:
+                sb[("e", n)] = work.tile([P, CM * P], F32, name="e")
+                sb[("o", n)] = opool.tile([P, P * CM], F32, name="o")
+            cols = slice(b * 4 * P, (b + 1) * 4 * P)
+            nc.vector.tensor_tensor(
+                out=sb[("e", n)][:, cols].rearrange("p (c j) -> p c j", c=4),
+                in0=sb[("d", n)][:, cols].rearrange("p (c j) -> p c j", c=4),
+                in1=sb[("rstd", n)][:, 0:P].unsqueeze(1).to_broadcast([P, 4, P]),
+                op=ALU.mult)
+
+        def gain_and_bias(n, b):
+            e = sb[("e", n)]
+            for c in range(4 * b, 4 * b + 4):
+                cols = slice(c * P, (c + 1) * P)
+                nc.scalar.activation(
+                    out=e[:, cols], in_=e[:, cols], func=ACT.Identity,
+                    scale=w32[:, c:c + 1], bias=b32[:, c:c + 1])
+
+        def lay_out(n, b):
+            cs = slice(4 * b, 4 * b + 4)
+            nc.gpsimd.tensor_scalar(
+                out=sb[("o", n)][:].rearrange("p (j c) -> p j c", c=CM)[:, :, cs],
+                in0=sb[("e", n)][:].rearrange("p (c j) -> p j c", c=CM)[:, :, cs],
+                scalar1=1.0, scalar2=0.0, op0=ALU.mult, op1=ALU.add)
+
         def scale_and_store(n):
             scale(n, 0)
             add_groups(n, 0, 1, nc.gpsimd, b32)
-            for b in range(1, 4):
+            for b in range(1, 3):
                 scale(n, b)
-            add_groups(n, 1, 4, nc.gpsimd, b32)
+            add_groups(n, 1, 3, nc.gpsimd, b32)
+            scale(n, 3)
+            add_groups(n, 3, 4, nc.gpsimd, b32)
             store(n)
 
         def last_add_and_store(n, b_ps):
@@ -267,9 +295,10 @@ def tile_trianglemultiplication_pa_t_kernel(tc, left, right, ln_c_w, ln_c_b, out
                 nc.vector.tensor_copy(out=w32[:], in_=w16[:])
                 nc.vector.tensor_copy(out=b32, in_=b16[:])
             co(u, [0])
-            tr(u, [2, 3])
+            tr(u, [2])
             if k >= 1:
                 bk(k - 1)
+            tr(u, [3])
             m1(k)
             for b in range(2):
                 t_mx(k, b)
@@ -327,10 +356,13 @@ def tile_trianglemultiplication_pa_t_kernel(tc, left, right, ln_c_w, ln_c_b, out
         for b in range(4):
             acc(n, b)
         rt(n)
-        for b in range(4):
+        for b in range(2):
+            scale_by_rstd(n - 1, b)
+            gain_and_bias(n - 1, b)
+        for b in range(2, 4):
             scale(n - 1, b)
-            if b < 2:
-                add_groups(n - 1, b, b + 1, nc.gpsimd, b32)
+        for b in range(2):
+            lay_out(n - 1, b)
         for b in range(2, 4):
             add_groups(n - 1, b, b + 1, nc.vector, b_ps)
         store(n - 1)

@@ -189,13 +189,13 @@ def tile_trianglemultiplication_pa_t_kernel(tc, left, right, ln_c_w, ln_c_b, out
                 sb[("rstd", n)] = ps_t.tile([P, 4 * P], F32, name="t_bank")
             nc.tensor.transpose(sb[("rstd", n)][:, 0:P], sb[("rstdT", n)][:], ident[:])
 
-        def scale(n, b):
+        def scale(n, b, channels=4):
             if ("e", n) not in sb:
                 sb[("e", n)] = work.tile([P, CM * P], F32, name="e")
                 sb[("o", n)] = opool.tile([P, P * CM], F32, name="o")
             rstd = sb[("rstd", n)][:, 0:P]
             e = sb[("e", n)]
-            for c in range(4 * b, 4 * b + 4):
+            for c in range(4 * b, 4 * b + channels):
                 cols = slice(c * P, (c + 1) * P)
                 nc.vector.scalar_tensor_tensor(
                     out=e[:, cols], in0=sb[("d", n)][:, cols], scalar=w32[:, c:c + 1], in1=rstd,
@@ -230,20 +230,34 @@ def tile_trianglemultiplication_pa_t_kernel(tc, left, right, ln_c_w, ln_c_b, out
                     out=e[:, cols], in_=e[:, cols], func=ACT.Identity,
                     scale=w32[:, c:c + 1], bias=b32[:, c:c + 1])
 
-        def lay_out(n, b):
+        def lay_out(n, b, on_scalar=False):
             cs = slice(4 * b, 4 * b + 4)
-            nc.gpsimd.tensor_scalar(
-                out=sb[("o", n)][:].rearrange("p (j c) -> p j c", c=CM)[:, :, cs],
-                in0=sb[("e", n)][:].rearrange("p (c j) -> p j c", c=CM)[:, :, cs],
-                scalar1=1.0, scalar2=0.0, op0=ALU.mult, op1=ALU.add)
+            o_jc = sb[("o", n)][:].rearrange("p (j c) -> p j c", c=CM)[:, :, cs]
+            e_jc = sb[("e", n)][:].rearrange("p (c j) -> p j c", c=CM)[:, :, cs]
+            if on_scalar:
+                nc.scalar.copy(out=o_jc, in_=e_jc)
+            else:
+                nc.gpsimd.tensor_scalar(
+                    out=o_jc, in0=e_jc, scalar1=1.0, scalar2=0.0, op0=ALU.mult, op1=ALU.add)
 
-        def scale_and_store(n):
+        def scale_first_groups(n):
             scale(n, 0)
             add_groups(n, 0, 1, nc.gpsimd, b32)
             for b in range(1, 3):
                 scale(n, b)
             add_groups(n, 1, 3, nc.gpsimd, b32)
-            scale(n, 3)
+
+        def scale_last_group(n):
+            scale(n, 3, 3)
+            cols = slice((CM - 1) * P, CM * P)
+            nc.vector.tensor_tensor(
+                out=sb[("e", n)][:, cols], in0=sb[("d", n)][:, cols], in1=sb[("rstd", n)][:, 0:P], op=ALU.mult)
+
+        def close(n):
+            cols = slice((CM - 1) * P, CM * P)
+            nc.vector.tensor_scalar(
+                out=sb[("e", n)][:, cols], in0=sb[("e", n)][:, cols],
+                scalar1=w32[:, CM - 1:CM], scalar2=None, op0=ALU.mult)
             add_groups(n, 3, 4, nc.gpsimd, b32)
             store(n)
 
@@ -252,16 +266,17 @@ def tile_trianglemultiplication_pa_t_kernel(tc, left, right, ln_c_w, ln_c_b, out
             e_jc = sb[("e", n)][:].rearrange("p (c j) -> p j c", c=CM)
             dram = out[n * P:(n + 1) * P].rearrange("i j c -> i (j c)")
             step = P // 4
+            cs = slice(0, 12)
             nc.gpsimd.tensor_tensor(
-                out=o_jc[:, 3 * step:], in0=e_jc[:, 3 * step:],
-                in1=b32.unsqueeze(1).to_broadcast([P, step, CM]), op=ALU.add)
+                out=o_jc[:, 3 * step:, cs], in0=e_jc[:, 3 * step:, cs],
+                in1=b32[:, cs].unsqueeze(1).to_broadcast([P, step, 12]), op=ALU.add)
             for piece in range(4):
                 js = slice(piece * step, (piece + 1) * step)
                 if piece == 3:
                     continue
                 nc.vector.tensor_tensor(
-                    out=o_jc[:, js], in0=e_jc[:, js],
-                    in1=b_ps.unsqueeze(1).to_broadcast([P, step, CM]), op=ALU.add)
+                    out=o_jc[:, js, cs], in0=e_jc[:, js, cs],
+                    in1=b_ps[:, cs].unsqueeze(1).to_broadcast([P, step, 12]), op=ALU.add)
                 if piece == 1:
                     nc.sync.dma_start(out=dram[:, 0:P * CM // 2], in_=sb[("o", n)][:, 0:P * CM // 2])
             nc.sync.dma_start(out=dram[:, P * CM // 2:], in_=sb[("o", n)][:, P * CM // 2:])
@@ -291,6 +306,8 @@ def tile_trianglemultiplication_pa_t_kernel(tc, left, right, ln_c_w, ln_c_b, out
             load(u + 3)
             quant(k + 2, 0)
             quant(k + 2, 1)
+            if k >= 2:
+                close(k - 2)
             if k == 1:
                 nc.vector.tensor_copy(out=w32[:], in_=w16[:])
                 nc.vector.tensor_copy(out=b32, in_=b16[:])
@@ -303,7 +320,8 @@ def tile_trianglemultiplication_pa_t_kernel(tc, left, right, ln_c_w, ln_c_b, out
             for b in range(2):
                 t_mx(k, b)
             if k >= 1:
-                scale_and_store(k - 1)
+                scale_first_groups(k - 1)
+                scale_last_group(k - 1)
             co(u, [1, 2])
             mean(k)
             co(u, [3])
@@ -327,6 +345,7 @@ def tile_trianglemultiplication_pa_t_kernel(tc, left, right, ln_c_w, ln_c_b, out
         n = N_TILES - 1
         quant(n + 1, 0)
         quant(n + 1, 1)
+        close(n - 3)
         turned = ps_tr.tile([P, 4 * P], F32, name="bank")
         nc.tensor.transpose(turned[:, 0:P], b_pad[:], ident[:])
         b_rows = small.tile([P, P], F32, name="b_rows")
@@ -348,7 +367,11 @@ def tile_trianglemultiplication_pa_t_kernel(tc, left, right, ln_c_w, ln_c_b, out
         for b in range(4):
             acc(n - 1, b)
         rt(n - 1)
-        scale_and_store(n - 2)
+        scale_by_rstd(n - 2, 3)
+        gain_and_bias(n - 2, 3)
+        scale_first_groups(n - 2)
+        lay_out(n - 2, 3)
+        store(n - 2)
         for b in range(4):
             centre(n, b)
             square(n, b)
@@ -361,12 +384,15 @@ def tile_trianglemultiplication_pa_t_kernel(tc, left, right, ln_c_w, ln_c_b, out
             gain_and_bias(n - 1, b)
         for b in range(2, 4):
             scale(n - 1, b)
-        for b in range(2):
-            lay_out(n - 1, b)
+        lay_out(n - 1, 0)
+        lay_out(n - 1, 1, on_scalar=True)
         for b in range(2, 4):
             add_groups(n - 1, b, b + 1, nc.vector, b_ps)
         store(n - 1)
         bk(n)
-        for b in range(4):
+        scale_by_rstd(n, 3)
+        gain_and_bias(n, 3)
+        for b in range(3):
             scale(n, b)
+        lay_out(n, 3, on_scalar=True)
         last_add_and_store(n, b_ps)

from contextlib import ExitStack

import concourse.mybir as mybir
from concourse.masks import make_identity

F32 = mybir.dt.float32
BF16 = mybir.dt.bfloat16
U32 = mybir.dt.uint32
U8 = mybir.dt.uint8
FP8X4 = mybir.dt.float8_e4m3fn_x4
ALU = mybir.AluOpType
ACT = mybir.ActivationFunctionType

NI, NJ, NK, CM = 1024, 128, 512, 16
EPS = 1e-5
P = 128
PACK = 4
CPAIRS = CM // 2
ROW = NK * CM
N_TILES = NI // P
N_UNITS = N_TILES + 1
CHUNK_I = P // PACK
CHUNKS = P // CHUNK_I
CHUNK_COLS = ROW // PACK
BANKS = 2 * CHUNKS
FLOPS = 2 * NI * NJ * NK * CM


def tile_trianglemultiplication_pa_t_kernel(tc, left, right, ln_c_w, ln_c_b, out):
    nc = tc.nc
    with ExitStack() as ctx:
        const = ctx.enter_context(tc.tile_pool(name="const", bufs=1))
        xpool = ctx.enter_context(tc.tile_pool(name="xpool", bufs=16))
        gpool = ctx.enter_context(tc.tile_pool(name="gpool", bufs=3))
        cpool = ctx.enter_context(tc.tile_pool(name="cpool", bufs=3))
        work = ctx.enter_context(tc.tile_pool(name="work", bufs=2))
        opool = ctx.enter_context(tc.tile_pool(name="opool", bufs=3))
        small = ctx.enter_context(tc.tile_pool(name="small", bufs=2))
        ps_tr = ctx.enter_context(tc.psum_pool(name="ps_tr", bufs=4))
        ps_t = ctx.enter_context(tc.psum_pool(name="ps_t", bufs=3))
        ps_s = ctx.enter_context(tc.psum_pool(name="ps_s", bufs=1))
        ctx.enter_context(tc.manual_schedule())

        w16 = const.tile([P, CM], BF16)
        b16 = const.tile([P, CM], BF16)
        eps_t = const.tile([P, 1], F32)
        nc.vector.memset(eps_t[:], EPS)
        warm = const.tile([P, 1], F32)
        nc.scalar.activation(out=warm[:], in_=eps_t[:], func=ACT.Abs_reciprocal_sqrt)
        ident = const.tile([P, P], F32)
        make_identity(nc, ident[:])
        w32 = const.tile([P, CM], F32)
        b_pad = const.tile([P, P], F32)
        nc.gpsimd.memset(b_pad[:], 0.0)
        b32 = b_pad[:, 0:CM]

        x_t = {}
        bank_t = {}
        grouped_t = {}
        codes_t = {}
        scales_t = {}
        stat_t = {}
        tb_t = {}
        sb = {}

        def load(u):
            if u >= N_UNITS:
                return
            rows = right if u == 0 else left[(u - 1) * P:u * P]
            for g in range(CHUNKS):
                x = xpool.tile([P, CHUNK_COLS], BF16, name="x")
                nc.sync.dma_start(
                    out=x[:],
                    in_=rows[g * CHUNK_I:(g + 1) * CHUNK_I].rearrange(
                        "i (t p) c -> (i t) (p c)", t=PACK))
                x_t[(u, g)] = x

        def tr(u, banks):
            if u >= N_UNITS:
                return
            for b in banks:
                g, hb = b // 2, b % 2
                words = x_t[(u, g)][:].bitcast(F32).rearrange("r (p q) -> r q p", q=CPAIRS)
                if u < 3 and b % 2 == 1:
                    bank = ps_t.tile([P, 4 * P], F32, name="t_bank")
                else:
                    bank = ps_tr.tile([P, 4 * P], F32, name="bank")
                for ql in range(4):
                    nc.tensor.transpose(
                        bank[:, ql * P:(ql + 1) * P], words[:, 4 * hb + ql, :], ident[:])
                bank_t[(u, b)] = bank

        def co(u, banks):
            if u >= N_UNITS:
                return
            for b in banks:
                g, hb = b // 2, b % 2
                if u not in grouped_t:
                    grouped_t[u] = gpool.tile([P, ROW], BF16, name="grouped", align_bytes=64)
                by_channel = grouped_t[u][:].rearrange("p (c x) -> p c x", c=CM)
                src = bank_t[(u, b)][:].bitcast(BF16).rearrange("p (q r e) -> p q e r", q=4, e=2)
                dst = by_channel[:, 8 * hb:8 * hb + 8, g * P:(g + 1) * P].rearrange(
                    "p (q e) r -> p q e r", e=2)
                on_vector = (b % 2 == 1) if u == 0 else (b in (3, 5, 7)) if u <= 2 else (b in (5, 7))
                if on_vector:
                    nc.vector.tensor_copy(out=dst, in_=src)
                else:
                    nc.scalar.copy(out=dst, in_=src)

        def quant(u, h):
            if u >= N_UNITS:
                return
            if h == 0:
                pool = const if u == 0 else cpool
                codes_t[u] = pool.tile([P, CM * P], U32, name="codes" if u else "r_codes", align_bytes=64)
                scales_t[u] = pool.tile([P, CM * P], U8, name="scales" if u else "r_scales", align_bytes=64)
            half = ROW // 2
            nc.vector.quantize_mx(
                out=codes_t[u][:, h * half // PACK:(h + 1) * half // PACK].bitcast(FP8X4),
                scales=scales_t[u][:, h * half // PACK:(h + 1) * half // PACK],
                in_=grouped_t[u][:, h * half:(h + 1) * half],
            )

        def mx(acc, n, c, start, stop):
            cols = slice(c * P, (c + 1) * P)
            nc.tensor.matmul_mx(
                out=acc,
                lhsT=codes_t[n + 1][:, cols].bitcast(FP8X4),
                lhsT_scale=scales_t[n + 1][:, cols],
                rhs=codes_t[0][:, cols].bitcast(FP8X4),
                rhs_scale=scales_t[0][:, cols],
                start=start,
                stop=stop,
            )

        def m1(n):
            if n == N_TILES - 1:
                stat_t[n] = ps_t.tile([P, 4 * P], F32, name="t_bank")
            else:
                stat_t[n] = ps_s.tile([P, 2 * P], F32, name="stat")
            for c in range(CM):
                mx(stat_t[n][:, 0:P], n, c, c == 0, c == CM - 1)

        def t_mx(n, b):
            if n >= N_TILES - 2:
                tb_t[(n, b)] = ps_tr.tile([P, 4 * P], F32, name="bank")
            else:
                tb_t[(n, b)] = ps_t.tile([P, 4 * P], F32, name="t_bank")
            for cc in range(4):
                mx(tb_t[(n, b)][:, cc * P:(cc + 1) * P], n, 4 * b + cc, True, True)

        def mean(n):
            sb[("mu", n)] = small.tile([P, P], F32, name="mu")
            nc.scalar.mul(out=sb[("mu", n)][:], in_=stat_t[n][:, 0:P], mul=1.0 / CM)

        def centre(n, b):
            if b == 0:
                sb[("d", n)] = work.tile([P, CM * P], F32, name="d")
            cols = slice(b * 4 * P, (b + 1) * 4 * P)
            nc.vector.tensor_tensor(
                out=sb[("d", n)][:, cols].rearrange("p (c j) -> p c j", c=4),
                in0=tb_t[(n, b)][:].rearrange("p (c j) -> p c j", c=4),
                in1=sb[("mu", n)][:].unsqueeze(1).to_broadcast([P, 4, P]),
                op=ALU.subtract,
            )

        def square(n, b):
            if b == 0:
                sb[("sq", n)] = work.tile([P, CM * P], F32, name="sq")
            cols = slice(b * 4 * P, (b + 1) * 4 * P)
            nc.scalar.activation(out=sb[("sq", n)][:, cols], in_=sb[("d", n)][:, cols], func=ACT.Square)

        def acc(n, b):
            for c in range(4 * b, 4 * b + 4):
                nc.tensor.matmul(
                    out=stat_t[n][:, P:2 * P], lhsT=sb[("sq", n)][:, c * P:(c + 1) * P], rhs=ident[:],
                    start=(c == 0), stop=(c == CM - 1), is_transpose=True)

        def rt(n):
            sb[("rstdT", n)] = small.tile([P, P], F32, name="rstdT")
            nc.scalar.activation(
                out=sb[("rstdT", n)][:], in_=stat_t[n][:, P:2 * P], func=ACT.Abs_reciprocal_sqrt,
                bias=eps_t[:], scale=1.0 / CM)

        def bk(n):
            if n == N_TILES - 1:
                sb[("rstd", n)] = sb[("rstd", n - 1)][:, P:3 * P]
            else:
                sb[("rstd", n)] = ps_t.tile([P, 4 * P], F32, name="t_bank")
            nc.tensor.transpose(sb[("rstd", n)][:, 0:P], sb[("rstdT", n)][:], ident[:])

        def scale(n, b, channels=4):
            if ("e", n) not in sb:
                sb[("e", n)] = work.tile([P, CM * P], F32, name="e")
                sb[("o", n)] = opool.tile([P, P * CM], F32, name="o")
            rstd = sb[("rstd", n)][:, 0:P]
            e = sb[("e", n)]
            for c in range(4 * b, 4 * b + channels):
                cols = slice(c * P, (c + 1) * P)
                nc.vector.scalar_tensor_tensor(
                    out=e[:, cols], in0=sb[("d", n)][:, cols], scalar=w32[:, c:c + 1], in1=rstd,
                    op0=ALU.mult, op1=ALU.mult)

        def add_groups(n, lo, hi, engine, bias):
            engine.tensor_tensor(
                out=sb[("o", n)][:].rearrange("p (j g c) -> p g j c", g=4, c=4)[:, lo:hi],
                in0=sb[("e", n)][:].rearrange("p (g c j) -> p g j c", g=4, c=4)[:, lo:hi],
                in1=bias.rearrange("p (g c) -> p g c", g=4)[:, lo:hi].unsqueeze(2).to_broadcast(
                    [P, hi - lo, P, 4]), op=ALU.add)

        def store(n):
            nc.sync.dma_start(out=out[n * P:(n + 1) * P].rearrange("i j c -> i (j c)"), in_=sb[("o", n)][:])

        def scale_by_rstd(n, b):
            if ("e", n) not in sb:
                sb[("e", n)] = work.tile([P, CM * P], F32, name="e")
                sb[("o", n)] = opool.tile([P, P * CM], F32, name="o")
            cols = slice(b * 4 * P, (b + 1) * 4 * P)
            nc.vector.tensor_tensor(
                out=sb[("e", n)][:, cols].rearrange("p (c j) -> p c j", c=4),
                in0=sb[("d", n)][:, cols].rearrange("p (c j) -> p c j", c=4),
                in1=sb[("rstd", n)][:, 0:P].unsqueeze(1).to_broadcast([P, 4, P]),
                op=ALU.mult)

        def gain_and_bias(n, b):
            e = sb[("e", n)]
            for c in range(4 * b, 4 * b + 4):
                cols = slice(c * P, (c + 1) * P)
                nc.scalar.activation(
                    out=e[:, cols], in_=e[:, cols], func=ACT.Identity,
                    scale=w32[:, c:c + 1], bias=b32[:, c:c + 1])

        def lay_out(n, b, on_scalar=False):
            cs = slice(4 * b, 4 * b + 4)
            o_jc = sb[("o", n)][:].rearrange("p (j c) -> p j c", c=CM)[:, :, cs]
            e_jc = sb[("e", n)][:].rearrange("p (c j) -> p j c", c=CM)[:, :, cs]
            if on_scalar:
                nc.scalar.copy(out=o_jc, in_=e_jc)
            else:
                nc.gpsimd.tensor_scalar(
                    out=o_jc, in0=e_jc, scalar1=1.0, scalar2=0.0, op0=ALU.mult, op1=ALU.add)

        def scale_first_groups(n):
            scale(n, 0)
            add_groups(n, 0, 1, nc.gpsimd, b32)
            for b in range(1, 3):
                scale(n, b)
            add_groups(n, 1, 3, nc.gpsimd, b32)

        def scale_last_group(n):
            scale(n, 3, 3)
            cols = slice((CM - 1) * P, CM * P)
            nc.vector.tensor_tensor(
                out=sb[("e", n)][:, cols], in0=sb[("d", n)][:, cols], in1=sb[("rstd", n)][:, 0:P], op=ALU.mult)

        def close(n):
            cols = slice((CM - 1) * P, CM * P)
            nc.vector.tensor_scalar(
                out=sb[("e", n)][:, cols], in0=sb[("e", n)][:, cols],
                scalar1=w32[:, CM - 1:CM], scalar2=None, op0=ALU.mult)
            add_groups(n, 3, 4, nc.gpsimd, b32)
            store(n)

        def last_add_and_store(n, b_ps):
            o_jc = sb[("o", n)][:].rearrange("p (j c) -> p j c", c=CM)
            e_jc = sb[("e", n)][:].rearrange("p (c j) -> p j c", c=CM)
            dram = out[n * P:(n + 1) * P].rearrange("i j c -> i (j c)")
            step = P // 4
            cs = slice(0, 12)
            nc.gpsimd.tensor_tensor(
                out=o_jc[:, 3 * step:, cs], in0=e_jc[:, 3 * step:, cs],
                in1=b32[:, cs].unsqueeze(1).to_broadcast([P, step, 12]), op=ALU.add)
            for piece in range(4):
                js = slice(piece * step, (piece + 1) * step)
                if piece == 3:
                    continue
                nc.vector.tensor_tensor(
                    out=o_jc[:, js, cs], in0=e_jc[:, js, cs],
                    in1=b_ps[:, cs].unsqueeze(1).to_broadcast([P, step, 12]), op=ALU.add)
                if piece == 1:
                    nc.sync.dma_start(out=dram[:, 0:P * CM // 2], in_=sb[("o", n)][:, 0:P * CM // 2])
            nc.sync.dma_start(out=dram[:, P * CM // 2:], in_=sb[("o", n)][:, P * CM // 2:])

        for u in range(4):
            load(u)
        for b in range(BANKS):
            tr(0, [b])
            co(0, [b])
        load(4)
        nc.scalar.dma_start(out=w16[:], in_=ln_c_w.partition_broadcast(P))
        nc.scalar.dma_start(out=b16[:], in_=ln_c_b.partition_broadcast(P))
        quant(0, 0)
        quant(0, 1)
        for b in range(BANKS):
            tr(1, [b])
            co(1, [b])
        load(5)
        quant(1, 0)
        quant(1, 1)
        for b in range(BANKS):
            tr(2, [b])
            co(2, [b])
        tr(3, [0, 1])
        for k in range(N_TILES - 2):
            u = k + 3
            load(u + 3)
            quant(k + 2, 0)
            quant(k + 2, 1)
            if k >= 2:
                close(k - 2)
            if k == 1:
                nc.vector.tensor_copy(out=w32[:], in_=w16[:])
                nc.vector.tensor_copy(out=b32, in_=b16[:])
            co(u, [0])
            tr(u, [2])
            if k >= 1:
                bk(k - 1)
            tr(u, [3])
            m1(k)
            for b in range(2):
                t_mx(k, b)
            if k >= 1:
                scale_first_groups(k - 1)
                scale_last_group(k - 1)
            co(u, [1, 2])
            mean(k)
            co(u, [3])
            tr(u, [4, 5])
            t_mx(k, 2)
            centre(k, 0)
            t_mx(k, 3)
            tr(u, [6, 7])
            co(u, [4])
            tr(u + 1, [0])
            square(k, 0)
            acc(k, 0)
            for b in range(1, 4):
                centre(k, b)
                square(k, b)
                acc(k, b)
            co(u, [5, 6, 7])
            rt(k)
            tr(u + 1, [1])

        n = N_TILES - 1
        quant(n + 1, 0)
        quant(n + 1, 1)
        close(n - 3)
        turned = ps_tr.tile([P, 4 * P], F32, name="bank")
        nc.tensor.transpose(turned[:, 0:P], b_pad[:], ident[:])
        b_rows = small.tile([P, P], F32, name="b_rows")
        nc.scalar.copy(out=b_rows[:], in_=turned[:, 0:P])
        bk(n - 2)
        m1(n - 1)
        for b in range(4):
            t_mx(n - 1, b)
        b_bank = ps_t.tile([P, 4 * P], F32, name="t_bank")
        nc.tensor.transpose(b_bank[:, 0:P], b_rows[:], ident[:])
        b_ps = b_bank[:, 0:CM]
        mean(n - 1)
        m1(n)
        for b in range(4):
            centre(n - 1, b)
            square(n - 1, b)
            t_mx(n, b)
        mean(n)
        for b in range(4):
            acc(n - 1, b)
        rt(n - 1)
        scale_by_rstd(n - 2, 3)
        gain_and_bias(n - 2, 3)
        scale_first_groups(n - 2)
        lay_out(n - 2, 3)
        store(n - 2)
        for b in range(4):
            centre(n, b)
            square(n, b)
        bk(n - 1)
        for b in range(4):
            acc(n, b)
        rt(n)
        for b in range(2):
            scale_by_rstd(n - 1, b)
            gain_and_bias(n - 1, b)
        for b in range(2, 4):
            scale(n - 1, b)
        lay_out(n - 1, 0)
        lay_out(n - 1, 1, on_scalar=True)
        for b in range(2, 4):
            add_groups(n - 1, b, b + 1, nc.vector, b_ps)
        store(n - 1)
        bk(n)
        scale_by_rstd(n, 3)
        gain_and_bias(n, 3)
        for b in range(3):
            scale(n, b)
        lay_out(n, 3, on_scalar=True)
        last_add_and_store(n, b_ps)
